import numpy as np
import ml_dtypes


def mxq(x, axis, fmt="e4m3"):
    dtype, down = {"e4m3": (ml_dtypes.float8_e4m3fn, 7), "e5m2": (ml_dtypes.float8_e5m2, 14)}[fmt]
    v = np.moveaxis(np.asarray(x, np.float32).astype(ml_dtypes.bfloat16).astype(np.float64), axis, -1)
    blocks = v.reshape(v.shape[:-1] + (-1, 32))
    amax = np.abs(blocks).max(-1, keepdims=True)
    byte = np.maximum(np.where(amax > 0, np.frexp(amax)[1] - 1 + 127, 0) - down, 1)
    scale = np.exp2(byte - 127.0)
    codes = (blocks / scale).astype(np.float32).astype(dtype).astype(np.float64)
    return np.moveaxis((codes * scale).reshape(v.shape), -1, axis)


WIDE = False


def mx_kscale(k):
    if not WIDE:
        return np.ones(k)
    levels = np.array([10, -10, 5, -5, 0])
    a = np.random.permutation(np.resize(levels, k // 512 * 4)).reshape(k // 512, 4)
    idx = np.arange(k)
    return np.exp2(a[idx // 512, idx % 128 // 32])


BF16 = ml_dtypes.bfloat16


def bf(x):
    return np.asarray(x, np.float32).astype(BF16)


def f64(x):
    return np.asarray(x).astype(np.float64)


B, D, O, M, R = 1024, 1024, 1024, 4, 8
SIGMA = 0.5


def draw(shape, p):
    z = np.random.standard_normal(shape + (R,))
    low = sum(z[..., r:r + 1] * p[r] for r in range(R))
    return 0.6 * low / np.sqrt(R * D) + 0.3 * np.random.standard_normal(shape + (D,)) / np.sqrt(D)


def setup_inputs():
    p = np.random.standard_normal((R, D))
    x = draw((B,), p)
    c = draw((O, M), p)
    t = mx_kscale(D)[np.arange(O) * D // O]
    g = np.maximum(t, 1.0 / t) ** 2
    c[np.arange(O), np.arange(O) % M] *= g[:, None]
    return {"x": bf(x), "centers": bf(c)}


def reference(x, centers):
    x, centers = f64(x), f64(centers)
    x2 = np.sum(x * x, axis=-1)
    c2 = np.sum(centers * centers, axis=-1)
    xc = (mxq(x, 1, "e4m3") @ mxq(centers, 2, "e4m3").reshape(O * M, D).T).reshape(B, O, M)
    d = x2[:, None, None] - 2.0 * xc + c2[None, :, :]
    probs = np.exp(-d / (2.0 * SIGMA * SIGMA))
    s = np.sum(probs, axis=-1)
    mx = np.max(probs, axis=-1)
    return s / (s + M - M * mx)

@@ -1,0 +1,231 @@
+import math
+
+import concourse.mybir as mybir
+from concourse.masks import make_identity
+
+F32 = mybir.dt.float32
+BF16 = mybir.dt.bfloat16
+U32 = mybir.dt.uint32
+U8 = mybir.dt.uint8
+FP8X4 = mybir.dt.float8_e4m3fn_x4
+ACT = mybir.ActivationFunctionType
+ALU = mybir.AluOpType
+AX = mybir.AxisListType
+
+P = 128
+B = 1024
+D = 1024
+O = 1024
+M = 4
+NJ = B // P
+NOB = O // P
+FLOPS = 2 * B * O * M * D
+
+SCALAR_COPIES = 0
+
+
+def tile_pnn_kernel(tc, x, centers, out):
+    nc = tc.nc
+    with tc.tile_pool(name="keep", bufs=1) as keep, tc.tile_pool(name="cin", bufs=3) as cin, tc.tile_pool(
+        name="cq", bufs=2
+    ) as cq, tc.tile_pool(name="pp", bufs=3) as pp, tc.tile_pool(name="tr", bufs=2) as tr, tc.tile_pool(
+        name="ot", bufs=3
+    ) as ot, tc.psum_pool(name="pmx", bufs=4) as pmx, tc.psum_pool(name="ptp", bufs=4) as ptp:
+        ident = keep.tile([P, P], F32)
+        make_identity(nc, ident[:])
+
+        x_nat = keep.tile([P, NJ * D], BF16, tag="xnat")
+        x_grp = keep.tile([P, 2 * B * 4], BF16, tag="xgrp", align_bytes=64)
+        x_codes = keep.tile([P, 2 * B], U32, align_bytes=64)
+        x_scales = keep.tile([P, 2 * B], U8, align_bytes=64)
+        s_all = keep.tile([P, NOB * B], F32)
+        u_all = keep.tile([P, NOB * B], F32)
+        junk = keep.tile([P, D], BF16)
+        x2 = keep.tile([P, NJ], F32)
+        c2 = keep.tile([P, NOB * M], F32)
+        nbias = keep.tile([P, NOB * M], F32)
+        w_row = keep.tile([P, NJ], F32)
+        xm = keep.tile([P, 1], F32)
+        rep = keep.tile([P, P], F32)
+        gmax = keep.tile([P, 1], F32)
+        nx2 = keep.tile([P, 1], F32)
+        wbias = keep.tile([P, 1], F32)
+
+        for jp in range(NJ // 2):
+            nc.sync.dma_start(
+                out=x_nat[:, jp * 2 * D : (jp + 1) * 2 * D].rearrange("p (j k) -> p j k", j=2),
+                in_=x[jp * 2 * P : (jp + 1) * 2 * P, :].rearrange("(j p) k -> p j k", p=P),
+            )
+
+        c_nats = {}
+
+        def load_c(ob):
+            c_nat = cin.tile([P, M * D], BF16)
+            nc.sync.dma_start(out=c_nat[:], in_=centers[ob * P : (ob + 1) * P].rearrange("p m k -> p (m k)"))
+            c_nats[ob] = c_nat
+
+        load_c(0)
+        load_c(1)
+
+        xw = x_nat[:].bitcast(F32)
+        xg32 = x_grp[:].bitcast(F32)
+        for j in range(NJ):
+            nc.scalar.activation(
+                out=junk[:], in_=x_nat[:, j * D : (j + 1) * D], func=ACT.Square, accum_out=x2[:, j : j + 1]
+            )
+        for hh in range(2):
+            for g in range(2):
+                for jq in range(2):
+                    jp = hh * 2 + jq
+                    tp = ptp.tile([P, 512], F32, tag="tp")
+                    for jj in range(2):
+                        for u in range(2):
+                            i = jj * 2 + u
+                            off = (2 * jp + jj) * 512 + 256 * g + 128 * u
+                            nc.tensor.transpose(out=tp[:, i * P : (i + 1) * P], in_=xw[:, off : off + P], identity=ident[:])
+                    base = g * 2048 + jp * 512
+                    nc.vector.tensor_copy(
+                        out=xg32[:, base : base + 512].rearrange("p (j r u) -> p j r u", j=2, u=2),
+                        in_=tp[:].rearrange("p (j u r) -> p j r u", j=2, u=2),
+                    )
+            for g in range(2):
+                nc.vector.quantize_mx(
+                    out=x_codes[:, g * B + hh * 512 : g * B + (hh + 1) * 512].bitcast(FP8X4),
+                    scales=x_scales[:, g * B + hh * 512 : g * B + (hh + 1) * 512],
+                    in_=x_grp[:, g * 4096 + hh * 2048 : g * 4096 + (hh + 1) * 2048],
+                )
+
+        nc.vector.reduce_max(out=xm[:], in_=x2[:], axis=AX.X)
+        nc.vector.tensor_copy(out=rep[:], in_=xm[:, 0:1].to_broadcast([P, P]))
+        tpx = ptp.tile([P, 512], F32, tag="tp")
+        nc.tensor.transpose(out=tpx[:, 0:P], in_=rep[:], identity=ident[:])
+        nc.vector.reduce_max(out=gmax[:], in_=tpx[:, 0:P], axis=AX.X)
+        nc.vector.tensor_scalar_mul(out=nx2[:], in0=gmax[:], scalar1=-2.0)
+        nc.vector.tensor_scalar(
+            out=wbias[:], in0=gmax[:], scalar1=-2.0, scalar2=math.log(4.0), op0=ALU.mult, op1=ALU.add
+        )
+        nc.scalar.activation(out=w_row[:], in_=x2[:], func=ACT.Exp, scale=2.0, bias=wbias[:, 0:1])
+        nc.vector.tensor_scalar_max(out=w_row[:], in0=w_row[:], scalar1=2.0 ** -60)
+
+        cqs = {}
+
+        def prep_c(ob):
+            c_nat = c_nats[ob]
+            cw = c_nat[:].bitcast(F32)
+            for m in range(M):
+                nc.scalar.activation(
+                    out=junk[:],
+                    in_=c_nat[:, m * D : (m + 1) * D],
+                    func=ACT.Square,
+                    accum_out=c2[:, ob * M + m : ob * M + m + 1],
+                )
+            nc.vector.tensor_scalar(
+                out=nbias[:, ob * M : (ob + 1) * M],
+                in0=c2[:, ob * M : (ob + 1) * M],
+                scalar1=-2.0,
+                scalar2=nx2[:, 0:1],
+                op0=ALU.mult,
+                op1=ALU.add,
+            )
+            c_grp = cq.tile([P, M * D], BF16, align_bytes=64)
+            c_codes = cq.tile([P, M * 2 * P], U32, align_bytes=64)
+            c_scales = cq.tile([P, M * 2 * P], U8, align_bytes=64)
+            cg32 = c_grp[:].bitcast(F32)
+            for m in range(M):
+                tp = ptp.tile([P, 512], F32, tag="tp")
+                for g in range(2):
+                    for u in range(2):
+                        i = g * 2 + u
+                        off = m * 512 + 256 * g + 128 * u
+                        nc.tensor.transpose(out=tp[:, i * P : (i + 1) * P], in_=cw[:, off : off + P], identity=ident[:])
+                dst = cg32[:, m * 512 : (m + 1) * 512].rearrange("p (g r u) -> p g r u", g=2, u=2)
+                src = tp[:].rearrange("p (g u r) -> p g r u", g=2, u=2)
+                if m < SCALAR_COPIES:
+                    nc.scalar.copy(out=dst, in_=src)
+                else:
+                    nc.vector.tensor_copy(out=dst, in_=src)
+            nc.vector.quantize_mx(out=c_codes[:].bitcast(FP8X4), scales=c_scales[:], in_=c_grp[:])
+            cqs[ob] = (c_codes, c_scales)
+
+        def main_c(ob, h):
+            c_codes, c_scales = cqs[ob]
+            p_t = pp.tile([P, M * 512], F32)
+            for m in range(M):
+                acc = pmx.tile([P, 512], F32, tag="acc")
+                for g in range(2):
+                    cs = slice((m * 2 + g) * P, (m * 2 + g + 1) * P)
+                    xs = slice(g * B + h * 512, g * B + (h + 1) * 512)
+                    nc.tensor.matmul_mx(
+                        out=acc[:],
+                        lhsT=c_codes[:, cs].bitcast(FP8X4),
+                        lhsT_scale=c_scales[:, cs],
+                        rhs=x_codes[:, xs].bitcast(FP8X4),
+                        rhs_scale=x_scales[:, xs],
+                        start=(g == 0),
+                        stop=(g == 1),
+                    )
+                nc.scalar.activation(
+                    out=p_t[:, m * 512 : (m + 1) * 512],
+                    in_=acc[:],
+                    func=ACT.Exp,
+                    scale=4.0,
+                    bias=nbias[:, ob * M + m : ob * M + m + 1],
+                )
+            t_max = tr.tile([P, 1024], F32)
+            t_sum = tr.tile([P, 1024], F32)
+            q_t = tr.tile([P, 512], F32)
+            sl = slice(ob * B + h * 512, ob * B + (h + 1) * 512)
+            nc.vector.tensor_tensor(out=t_max[:], in0=p_t[:, 0:1024], in1=p_t[:, 1024:2048], op=ALU.max)
+            nc.vector.tensor_tensor(out=t_sum[:], in0=p_t[:, 0:1024], in1=p_t[:, 1024:2048], op=ALU.add)
+            nc.vector.tensor_tensor(out=q_t[:], in0=t_max[:, 0:512], in1=t_max[:, 512:1024], op=ALU.max)
+            nc.vector.tensor_tensor(out=s_all[:, sl], in0=t_sum[:, 0:512], in1=t_sum[:, 512:1024], op=ALU.add)
+            nc.vector.scalar_tensor_tensor(
+                out=u_all[:, sl], in0=q_t[:], scalar=-4.0, in1=s_all[:, sl], op0=ALU.mult, op1=ALU.add
+            )
+
+        prep_c(0)
+        for ob in range(NOB - 1):
+            if ob + 2 < NOB:
+                load_c(ob + 2)
+            prep_c(ob + 1)
+            main_c(ob, 0)
+            main_c(ob, 1)
+
+        with tc.manual_schedule():
+            main_c(NOB - 1, 0)
+            main_c(NOB - 1, 1)
+
+            l_a = keep.tile([P, 4 * O], F32, tag="xnat")
+            l_b = keep.tile([P, 4 * O], F32, tag="xgrp", align_bytes=64)
+
+            def l_view(j, oh):
+                l_t = l_a if j < 4 else l_b
+                return l_t[:, (j % 4) * O + oh * 512 : (j % 4) * O + (oh + 1) * 512]
+
+            for oh in range(2):
+                for j in range(NJ):
+                    tp = ptp.tile([P, 512], F32, tag="tp")
+                    for i in range(4):
+                        ob = oh * 4 + i
+                        nc.tensor.transpose(
+                            out=tp[:, i * P : (i + 1) * P],
+                            in_=u_all[:, ob * B + j * P : ob * B + (j + 1) * P],
+                            identity=ident[:],
+                        )
+                    nc.scalar.activation(out=l_view(j, oh), in_=tp[:], func=ACT.Ln, bias=w_row[:, j : j + 1])
+            for j in range(NJ):
+                o_t = ot.tile([P, O], F32)
+                for oh in range(2):
+                    acc = pmx.tile([P, 512], F32, tag="acc")
+                    for i in range(4):
+                        ob = oh * 4 + i
+                        nc.tensor.transpose(
+                            out=acc[:, i * P : (i + 1) * P],
+                            in_=s_all[:, ob * B + j * P : ob * B + (j + 1) * P],
+                            identity=ident[:],
+                        )
+                    nc.scalar.activation(out=l_view(j, oh), in_=l_view(j, oh), func=ACT.Exp, scale=-1.0)
+                    nc.vector.tensor_tensor(
+                        out=o_t[:, oh * 512 : (oh + 1) * 512], in0=acc[:], in1=l_view(j, oh), op=ALU.mult
+                    )
+                nc.sync.dma_start(out=out[j * P : (j + 1) * P, :], in_=o_t[:])

@@ -19,18 +19,21 @@ O = 1024
 M = 4
 NJ = B // P
 NOB = O // P
+NU = 2 * NOB
+H = 512
 FLOPS = 2 * B * O * M * D
-
-SCALAR_COPIES = 0
+THREE = (1, 2, 3)
 
 
 def tile_pnn_kernel(tc, x, centers, out):
     nc = tc.nc
     with tc.tile_pool(name="keep", bufs=1) as keep, tc.tile_pool(name="cin", bufs=3) as cin, tc.tile_pool(
         name="cq", bufs=2
-    ) as cq, tc.tile_pool(name="pp", bufs=3) as pp, tc.tile_pool(name="tr", bufs=2) as tr, tc.tile_pool(
+    ) as cq, tc.tile_pool(name="pp", bufs=4) as pp, tc.tile_pool(name="tr", bufs=2) as tr, tc.tile_pool(
         name="ot", bufs=3
-    ) as ot, tc.psum_pool(name="pmx", bufs=4) as pmx, tc.psum_pool(name="ptp", bufs=4) as ptp:
+    ) as ot, tc.psum_pool(name="pmx", bufs=4) as pmx, tc.psum_pool(name="ptp", bufs=3) as ptp, tc.psum_pool(
+        name="pgr", bufs=1
+    ) as pgr, tc.manual_schedule():
         ident = keep.tile([P, P], F32)
         make_identity(nc, ident[:])
 
@@ -39,122 +42,171 @@ def tile_pnn_kernel(tc, x, centers, out):
         x_codes = keep.tile([P, 2 * B], U32, align_bytes=64)
         x_scales = keep.tile([P, 2 * B], U8, align_bytes=64)
         s_all = keep.tile([P, NOB * B], F32)
-        u_all = keep.tile([P, NOB * B], F32)
+        q_all = keep.tile([P, NOB * B], F32)
         junk = keep.tile([P, D], BF16)
+        junk_g = keep.tile([P, P], F32)
         x2 = keep.tile([P, NJ], F32)
         c2 = keep.tile([P, NOB * M], F32)
-        nbias = keep.tile([P, NOB * M], F32)
+        nbias = keep.tile([P, 2 * NOB * M], F32)
         w_row = keep.tile([P, NJ], F32)
-        xm = keep.tile([P, 1], F32)
-        rep = keep.tile([P, P], F32)
-        gmax = keep.tile([P, 1], F32)
-        nx2 = keep.tile([P, 1], F32)
-        wbias = keep.tile([P, 1], F32)
+        xm = keep.tile([P, 2], F32)
+        gmax = keep.tile([P, 2], F32)
+        nx2 = keep.tile([P, 2], F32)
+        wbias = keep.tile([P, 2], F32)
 
-        for jp in range(NJ // 2):
+        c_nats = {}
+        c_grps = {}
+        c_qs = {}
+        p_ts = {}
+
+        def load_x(jp):
             nc.sync.dma_start(
                 out=x_nat[:, jp * 2 * D : (jp + 1) * 2 * D].rearrange("p (j k) -> p j k", j=2),
                 in_=x[jp * 2 * P : (jp + 1) * 2 * P, :].rearrange("(j p) k -> p j k", p=P),
             )
 
-        c_nats = {}
-
-        def load_c(ob):
+        def load_c(ob, pieces=1):
             c_nat = cin.tile([P, M * D], BF16)
-            nc.sync.dma_start(out=c_nat[:], in_=centers[ob * P : (ob + 1) * P].rearrange("p m k -> p (m k)"))
+            n = M // pieces
+            for i in range(pieces):
+                nc.sync.dma_start(
+                    out=c_nat[:, i * n * D : (i + 1) * n * D].rearrange("p (m k) -> p m k", m=n),
+                    in_=centers[ob * P : (ob + 1) * P, i * n : (i + 1) * n, :],
+                )
             c_nats[ob] = c_nat
-
-        load_c(0)
-        load_c(1)
 
         xw = x_nat[:].bitcast(F32)
         xg32 = x_grp[:].bitcast(F32)
-        for j in range(NJ):
-            nc.scalar.activation(
-                out=junk[:], in_=x_nat[:, j * D : (j + 1) * D], func=ACT.Square, accum_out=x2[:, j : j + 1]
+
+        def bank(pool, tag):
+            b_t = pool.tile([P, 512], F32, tag=tag)
+            return b_t
+
+        def turn_x(jp, g, tp, copy):
+            for jj in range(2):
+                for u in range(2):
+                    i = jj * 2 + u
+                    off = (2 * jp + jj) * 512 + 256 * g + 128 * u
+                    nc.tensor.transpose(out=tp[:, i * P : (i + 1) * P], in_=xw[:, off : off + P], identity=ident[:])
+            base = g * 2048 + jp * 512
+            copy(
+                out=xg32[:, base : base + 512].rearrange("p (j r u) -> p j r u", j=2, u=2),
+                in_=tp[:].rearrange("p (j u r) -> p j r u", j=2, u=2),
             )
-        for hh in range(2):
-            for g in range(2):
-                for jq in range(2):
-                    jp = hh * 2 + jq
-                    tp = ptp.tile([P, 512], F32, tag="tp")
-                    for jj in range(2):
-                        for u in range(2):
-                            i = jj * 2 + u
-                            off = (2 * jp + jj) * 512 + 256 * g + 128 * u
-                            nc.tensor.transpose(out=tp[:, i * P : (i + 1) * P], in_=xw[:, off : off + P], identity=ident[:])
-                    base = g * 2048 + jp * 512
-                    nc.vector.tensor_copy(
-                        out=xg32[:, base : base + 512].rearrange("p (j r u) -> p j r u", j=2, u=2),
-                        in_=tp[:].rearrange("p (j u r) -> p j r u", j=2, u=2),
-                    )
-            for g in range(2):
-                nc.vector.quantize_mx(
-                    out=x_codes[:, g * B + hh * 512 : g * B + (hh + 1) * 512].bitcast(FP8X4),
-                    scales=x_scales[:, g * B + hh * 512 : g * B + (hh + 1) * 512],
-                    in_=x_grp[:, g * 4096 + hh * 2048 : g * 4096 + (hh + 1) * 2048],
-                )
 
-        nc.vector.reduce_max(out=xm[:], in_=x2[:], axis=AX.X)
-        nc.vector.tensor_copy(out=rep[:], in_=xm[:, 0:1].to_broadcast([P, P]))
-        tpx = ptp.tile([P, 512], F32, tag="tp")
-        nc.tensor.transpose(out=tpx[:, 0:P], in_=rep[:], identity=ident[:])
-        nc.vector.reduce_max(out=gmax[:], in_=tpx[:, 0:P], axis=AX.X)
-        nc.vector.tensor_scalar_mul(out=nx2[:], in0=gmax[:], scalar1=-2.0)
-        nc.vector.tensor_scalar(
-            out=wbias[:], in0=gmax[:], scalar1=-2.0, scalar2=math.log(4.0), op0=ALU.mult, op1=ALU.add
-        )
-        nc.scalar.activation(out=w_row[:], in_=x2[:], func=ACT.Exp, scale=2.0, bias=wbias[:, 0:1])
-        nc.vector.tensor_scalar_max(out=w_row[:], in0=w_row[:], scalar1=2.0 ** -60)
+        def quant_x(h, g):
+            cols = slice(g * B + h * H, g * B + (h + 1) * H)
+            nc.vector.quantize_mx(
+                out=x_codes[:, cols].bitcast(FP8X4),
+                scales=x_scales[:, cols],
+                in_=x_grp[:, 4 * (g * B + h * H) : 4 * (g * B + (h + 1) * H)],
+            )
 
-        cqs = {}
+        def square(src, acc):
+            nc.scalar.activation(out=junk[:], in_=src, func=ACT.Square, accum_out=acc)
 
-        def prep_c(ob):
-            c_nat = c_nats[ob]
-            cw = c_nat[:].bitcast(F32)
-            for m in range(M):
-                nc.scalar.activation(
-                    out=junk[:],
-                    in_=c_nat[:, m * D : (m + 1) * D],
-                    func=ACT.Square,
-                    accum_out=c2[:, ob * M + m : ob * M + m + 1],
-                )
+        def gram(views, dst):
+            for i, v in enumerate(views):
+                nc.tensor.matmul(out=dst, lhsT=v, rhs=v, start=(i == 0), stop=(i == len(views) - 1))
+
+        def diagonal(src, acc):
+            nc.vector.scalar_tensor_tensor(
+                out=junk_g[:], in0=src, scalar=1.0, in1=ident[:], op0=ALU.mult, op1=ALU.mult, accum_out=acc
+            )
+
+        def shift(h, tpx):
+            rep = tr.tile([P, P], F32)
+            nc.vector.reduce_max(out=xm[:, h : h + 1], in_=x2[:, 4 * h : 4 * h + 4], axis=AX.X)
+            nc.vector.tensor_copy(out=rep[:], in_=xm[:, h : h + 1].to_broadcast([P, P]))
+            nc.tensor.transpose(out=tpx[:, 0:P], in_=rep[:], identity=ident[:])
+            nc.vector.reduce_max(out=gmax[:, h : h + 1], in_=tpx[:, 0:P], axis=AX.X)
+            nc.vector.tensor_scalar_mul(out=nx2[:, h : h + 1], in0=gmax[:, h : h + 1], scalar1=-2.0)
+
+        def row_weights(h):
             nc.vector.tensor_scalar(
-                out=nbias[:, ob * M : (ob + 1) * M],
-                in0=c2[:, ob * M : (ob + 1) * M],
+                out=wbias[:, h : h + 1],
+                in0=gmax[:, h : h + 1],
                 scalar1=-2.0,
-                scalar2=nx2[:, 0:1],
+                scalar2=math.log(4.0),
                 op0=ALU.mult,
                 op1=ALU.add,
             )
+            js = slice(4 * h, 4 * h + 4)
+            nc.scalar.activation(out=w_row[:, js], in_=x2[:, js], func=ACT.Exp, scale=2.0, bias=wbias[:, h : h + 1])
+            nc.vector.tensor_scalar_max(out=w_row[:, js], in0=w_row[:, js], scalar1=2.0**-60)
+
+        def turn_c(ob, m, copy):
+            cw = c_nats[ob][:].bitcast(F32)
+            tp = ptp.tile([P, 512], F32, tag="tp")
+            for g in range(2):
+                for u in range(2):
+                    i = g * 2 + u
+                    off = m * 512 + 256 * g + 128 * u
+                    nc.tensor.transpose(out=tp[:, i * P : (i + 1) * P], in_=cw[:, off : off + P], identity=ident[:])
+            cg32 = c_grps[ob][:].bitcast(F32)
+            copy(
+                out=cg32[:, m * 512 : (m + 1) * 512].rearrange("p (g r u) -> p g r u", g=2, u=2),
+                in_=tp[:].rearrange("p (g u r) -> p g r u", g=2, u=2),
+            )
+
+        def new_c(ob):
             c_grp = cq.tile([P, M * D], BF16, align_bytes=64)
             c_codes = cq.tile([P, M * 2 * P], U32, align_bytes=64)
             c_scales = cq.tile([P, M * 2 * P], U8, align_bytes=64)
-            cg32 = c_grp[:].bitcast(F32)
-            for m in range(M):
-                tp = ptp.tile([P, 512], F32, tag="tp")
-                for g in range(2):
-                    for u in range(2):
-                        i = g * 2 + u
-                        off = m * 512 + 256 * g + 128 * u
-                        nc.tensor.transpose(out=tp[:, i * P : (i + 1) * P], in_=cw[:, off : off + P], identity=ident[:])
-                dst = cg32[:, m * 512 : (m + 1) * 512].rearrange("p (g r u) -> p g r u", g=2, u=2)
-                src = tp[:].rearrange("p (g u r) -> p g r u", g=2, u=2)
-                if m < SCALAR_COPIES:
-                    nc.scalar.copy(out=dst, in_=src)
-                else:
-                    nc.vector.tensor_copy(out=dst, in_=src)
-            nc.vector.quantize_mx(out=c_codes[:].bitcast(FP8X4), scales=c_scales[:], in_=c_grp[:])
-            cqs[ob] = (c_codes, c_scales)
+            c_grps[ob] = c_grp
+            c_qs[ob] = (c_codes, c_scales)
 
-        def main_c(ob, h):
-            c_codes, c_scales = cqs[ob]
-            p_t = pp.tile([P, M * 512], F32)
+        def quant_c(ob, hf):
+            c_codes, c_scales = c_qs[ob]
+            cols = slice(hf * 512, (hf + 1) * 512)
+            nc.vector.quantize_mx(
+                out=c_codes[:, cols].bitcast(FP8X4),
+                scales=c_scales[:, cols],
+                in_=c_grps[ob][:, hf * 2048 : (hf + 1) * 2048],
+            )
+
+        def square_c(ob, m):
+            square(c_nats[ob][:, m * D : (m + 1) * D], c2[:, ob * M + m : ob * M + m + 1])
+
+        def gram_c(ob, ms, gr):
+            for i, m in enumerate(ms):
+                col = c_grps[ob][:, m * D : (m + 1) * D].rearrange("p (g r t) -> p g t r", g=2, t=4)
+                gram([col[:, g, t, :] for g in range(2) for t in range(4)], gr[:, i * P : (i + 1) * P])
+            for i, m in enumerate(ms):
+                diagonal(gr[:, i * P : (i + 1) * P], c2[:, ob * M + m : ob * M + m + 1])
+
+        def gram_x(js, gr):
+            for i, j in enumerate(js):
+                views = []
+                for g in range(2):
+                    a = g * 4 * B + j * 512
+                    col = x_grp[:, a : a + 512].rearrange("p (r t) -> p t r", t=4)
+                    views += [col[:, t, :] for t in range(4)]
+                gram(views, gr[:, i * P : (i + 1) * P])
+            for i, j in enumerate(js):
+                diagonal(gr[:, i * P : (i + 1) * P], x2[:, j : j + 1])
+
+        def biases(ob, h):
+            a = h * NOB * M + ob * M
+            nc.vector.tensor_scalar(
+                out=nbias[:, a : a + M],
+                in0=c2[:, ob * M : (ob + 1) * M],
+                scalar1=-2.0,
+                scalar2=nx2[:, h : h + 1],
+                op0=ALU.mult,
+                op1=ALU.add,
+            )
+
+        def products(k):
+            ob, h = k // 2, k % 2
+            c_codes, c_scales = c_qs[ob]
+            p_t = pp.tile([P, M * H], F32)
+            p_ts[k] = p_t
             for m in range(M):
                 acc = pmx.tile([P, 512], F32, tag="acc")
                 for g in range(2):
                     cs = slice((m * 2 + g) * P, (m * 2 + g + 1) * P)
-                    xs = slice(g * B + h * 512, g * B + (h + 1) * 512)
+                    xs = slice(g * B + h * H, g * B + (h + 1) * H)
                     nc.tensor.matmul_mx(
                         out=acc[:],
                         lhsT=c_codes[:, cs].bitcast(FP8X4),
@@ -164,68 +216,141 @@ def tile_pnn_kernel(tc, x, centers, out):
                         start=(g == 0),
                         stop=(g == 1),
                     )
+                a = h * NOB * M + ob * M + m
                 nc.scalar.activation(
-                    out=p_t[:, m * 512 : (m + 1) * 512],
-                    in_=acc[:],
-                    func=ACT.Exp,
-                    scale=4.0,
-                    bias=nbias[:, ob * M + m : ob * M + m + 1],
+                    out=p_t[:, m * H : (m + 1) * H], in_=acc[:], func=ACT.Exp, scale=4.0, bias=nbias[:, a : a + 1]
                 )
-            t_max = tr.tile([P, 1024], F32)
-            t_sum = tr.tile([P, 1024], F32)
-            q_t = tr.tile([P, 512], F32)
-            sl = slice(ob * B + h * 512, ob * B + (h + 1) * 512)
-            nc.vector.tensor_tensor(out=t_max[:], in0=p_t[:, 0:1024], in1=p_t[:, 1024:2048], op=ALU.max)
-            nc.vector.tensor_tensor(out=t_sum[:], in0=p_t[:, 0:1024], in1=p_t[:, 1024:2048], op=ALU.add)
-            nc.vector.tensor_tensor(out=q_t[:], in0=t_max[:, 0:512], in1=t_max[:, 512:1024], op=ALU.max)
-            nc.vector.tensor_tensor(out=s_all[:, sl], in0=t_sum[:, 0:512], in1=t_sum[:, 512:1024], op=ALU.add)
-            nc.vector.scalar_tensor_tensor(
-                out=u_all[:, sl], in0=q_t[:], scalar=-4.0, in1=s_all[:, sl], op0=ALU.mult, op1=ALU.add
-            )
 
-        prep_c(0)
-        for ob in range(NOB - 1):
-            if ob + 2 < NOB:
-                load_c(ob + 2)
-            prep_c(ob + 1)
-            main_c(ob, 0)
-            main_c(ob, 1)
+        def tree(k, between=()):
+            ob, h = k // 2, k % 2
+            p_t = p_ts[k]
+            sl = slice(ob * B + h * H, ob * B + (h + 1) * H)
+            todo = list(between)
+            t_max = tr.tile([P, 2 * H], F32)
+            t_sum = tr.tile([P, 2 * H], F32)
+            q_t = tr.tile([P, H], F32)
+            nc.vector.tensor_tensor(out=t_max[:], in0=p_t[:, 0 : 2 * H], in1=p_t[:, 2 * H : 4 * H], op=ALU.max)
+            nc.vector.tensor_tensor(out=t_sum[:], in0=p_t[:, 0 : 2 * H], in1=p_t[:, 2 * H : 4 * H], op=ALU.add)
+            for f in todo:
+                f()
+            nc.vector.tensor_tensor(out=q_t[:], in0=t_max[:, 0:H], in1=t_max[:, H : 2 * H], op=ALU.max)
+            nc.vector.tensor_tensor(out=s_all[:, sl], in0=t_sum[:, 0:H], in1=t_sum[:, H : 2 * H], op=ALU.add)
+            nc.vector.tensor_scalar_mul(out=q_all[:, sl], in0=q_t[:], scalar1=-4.0)
 
-        with tc.manual_schedule():
-            main_c(NOB - 1, 0)
-            main_c(NOB - 1, 1)
+        load_x(0)
+        load_x(1)
+        load_c(0, pieces=2)
+        load_x(2)
+        load_x(3)
+        load_c(1, pieces=2)
+        load_c(2)
+        for j in range(3):
+            square(x_nat[:, j * D : (j + 1) * D], x2[:, j : j + 1])
+        for jp in range(2):
+            for g in range(2):
+                turn_x(jp, g, bank(pmx, "acc"), nc.vector.tensor_copy)
+        for g in range(2):
+            quant_x(0, g)
+        new_c(0)
+        for m in range(M):
+            turn_c(0, m, nc.scalar.copy)
+        gram_x([3], bank(pgr, "gr"))
+        quant_c(0, 0)
+        shift(0, bank(pmx, "acc"))
+        square_c(0, 0)
+        gram_c(0, [1, 2, 3], bank(pmx, "acc"))
+        quant_c(0, 1)
+        biases(0, 0)
+        for jp in range(2, 4):
+            for g in range(2):
+                turn_x(jp, g, bank(ptp, "tp"), nc.scalar.copy if jp == 2 else nc.vector.tensor_copy)
+        for g in range(2):
+            quant_x(1, g)
+        products(0)
+        gram_x([4, 5, 6, 7], bank(pgr, "gr"))
+        new_c(1)
+        turn_c(1, 0, nc.scalar.copy)
+        turn_c(1, 1, nc.scalar.copy)
+        shift(1, bank(pmx, "acc"))
+        biases(0, 1)
+        square_c(1, 0)
 
-            l_a = keep.tile([P, 4 * O], F32, tag="xnat")
-            l_b = keep.tile([P, 4 * O], F32, tag="xgrp", align_bytes=64)
+        def turn_step(k):
+            hf = (k + 1) % 2
+            ob = (k + 3 - hf) // 2
+            if ob >= NOB:
+                return
+            if hf == 0:
+                new_c(ob)
+            if not (hf and ob in THREE):
+                square_c(ob, 2 * hf)
+            turn_c(ob, 2 * hf, nc.scalar.copy)
+            turn_c(ob, 2 * hf + 1, nc.scalar.copy)
 
-            def l_view(j, oh):
-                l_t = l_a if j < 4 else l_b
-                return l_t[:, (j % 4) * O + oh * 512 : (j % 4) * O + (oh + 1) * 512]
+        def quant_step(k):
+            hf = k % 2
+            ob = (k + 2 - hf) // 2
+            if ob >= NOB:
+                return
+            quant_c(ob, hf)
+            gram_c(ob, [2, 3] if hf and ob in THREE else [2 * hf + 1], bank(pgr, "gr"))
+            if hf == 1:
+                biases(ob, 0)
+                biases(ob, 1)
 
-            for oh in range(2):
-                for j in range(NJ):
-                    tp = ptp.tile([P, 512], F32, tag="tp")
-                    for i in range(4):
-                        ob = oh * 4 + i
-                        nc.tensor.transpose(
-                            out=tp[:, i * P : (i + 1) * P],
-                            in_=u_all[:, ob * B + j * P : ob * B + (j + 1) * P],
-                            identity=ident[:],
-                        )
-                    nc.scalar.activation(out=l_view(j, oh), in_=tp[:], func=ACT.Ln, bias=w_row[:, j : j + 1])
-            for j in range(NJ):
-                o_t = ot.tile([P, O], F32)
-                for oh in range(2):
-                    acc = pmx.tile([P, 512], F32, tag="acc")
-                    for i in range(4):
-                        ob = oh * 4 + i
-                        nc.tensor.transpose(
-                            out=acc[:, i * P : (i + 1) * P],
-                            in_=s_all[:, ob * B + j * P : ob * B + (j + 1) * P],
-                            identity=ident[:],
-                        )
-                    nc.scalar.activation(out=l_view(j, oh), in_=l_view(j, oh), func=ACT.Exp, scale=-1.0)
-                    nc.vector.tensor_tensor(
-                        out=o_t[:, oh * 512 : (oh + 1) * 512], in0=acc[:], in1=l_view(j, oh), op=ALU.mult
+        for k in range(NU):
+            if k % 2 == 0 and k // 2 + 3 < NOB:
+                load_c(k // 2 + 3)
+            if k == 0:
+                quant_step(0)
+                turn_step(0)
+            else:
+                turn_step(k)
+                tree(k - 1, [lambda: quant_step(k)])
+                products(k)
+            if k in (2, 3):
+                row_weights(k - 2)
+
+        l_a = keep.tile([P, 4 * O], F32, tag="xnat")
+        l_b = keep.tile([P, 4 * O], F32, tag="xgrp", align_bytes=64)
+
+        def l_view(j, a, b):
+            l_t = l_a if j < 4 else l_b
+            return l_t[:, (j % 4) * O + a : (j % 4) * O + b]
+
+        def back(dst, srcs, j, oh):
+            for i in range(4):
+                ob = oh * 4 + i
+                for n, t in enumerate(srcs):
+                    nc.tensor.matmul(
+                        out=dst[:, i * P : (i + 1) * P],
+                        lhsT=t[:, ob * B + j * P : ob * B + (j + 1) * P],
+                        rhs=ident[:],
+                        is_transpose=True,
+                        start=(n == 0),
+                        stop=(n == len(srcs) - 1),
                     )
+
+        for oh in range(2):
+            if oh == 1:
+                tree(NU - 1)
+            for j in range(NJ):
+                tp = bank(ptp, "tp")
+                back(tp, (s_all, q_all), j, oh)
+                nc.scalar.activation(
+                    out=l_view(j, oh * H, (oh + 1) * H), in_=tp[:], func=ACT.Ln, bias=w_row[:, j : j + 1]
+                )
+        for j in range(NJ):
+            o_t = ot.tile([P, O], F32)
+            for oh in range(2):
+                l_h = l_view(j, oh * H, (oh + 1) * H)
+                nc.scalar.activation(out=l_h, in_=l_h, func=ACT.Exp, scale=-1.0)
+                acc = bank(pmx, "acc")
+                back(acc, (s_all,), j, oh)
+                nc.vector.tensor_tensor(out=o_t[:, oh * H : (oh + 1) * H], in0=acc[:], in1=l_h, op=ALU.mult)
+                if j == NJ - 1:
+                    nc.sync.dma_start(
+                        out=out[j * P : (j + 1) * P, oh * H : (oh + 1) * H], in_=o_t[:, oh * H : (oh + 1) * H]
+                    )
+            if j < NJ - 1:
                 nc.sync.dma_start(out=out[j * P : (j + 1) * P, :], in_=o_t[:])

@@ -22,16 +22,14 @@ NOB = O // P
 NU = 2 * NOB
 H = 512
 FLOPS = 2 * B * O * M * D
-THREE = (1, 2, 3)
+SCALE = (1.0, 1.0, 4.0, 4.0)
 
 
 def tile_pnn_kernel(tc, x, centers, out):
     nc = tc.nc
     with tc.tile_pool(name="keep", bufs=1) as keep, tc.tile_pool(name="cin", bufs=3) as cin, tc.tile_pool(
-        name="cq", bufs=2
-    ) as cq, tc.tile_pool(name="pp", bufs=4) as pp, tc.tile_pool(name="tr", bufs=2) as tr, tc.tile_pool(
-        name="ot", bufs=3
-    ) as ot, tc.psum_pool(name="pmx", bufs=4) as pmx, tc.psum_pool(name="ptp", bufs=3) as ptp, tc.psum_pool(
+        name="cq", bufs=3
+    ) as cq, tc.tile_pool(name="cg", bufs=2) as cg, tc.tile_pool(name="pp", bufs=4) as pp, tc.tile_pool(name="tr", bufs=2) as tr, tc.psum_pool(name="pmx", bufs=4) as pmx, tc.psum_pool(name="ptp", bufs=3) as ptp, tc.psum_pool(
         name="pgr", bufs=1
     ) as pgr, tc.manual_schedule():
         ident = keep.tile([P, P], F32)
@@ -44,6 +42,7 @@ def tile_pnn_kernel(tc, x, centers, out):
         s_all = keep.tile([P, NOB * B], F32)
         q_all = keep.tile([P, NOB * B], F32)
         junk = keep.tile([P, D], BF16)
+        junk_v = keep.tile([P, D], BF16)
         junk_g = keep.tile([P, P], F32)
         x2 = keep.tile([P, NJ], F32)
         c2 = keep.tile([P, NOB * M], F32)
@@ -51,8 +50,7 @@ def tile_pnn_kernel(tc, x, centers, out):
         w_row = keep.tile([P, NJ], F32)
         xm = keep.tile([P, 2], F32)
         gmax = keep.tile([P, 2], F32)
-        nx2 = keep.tile([P, 2], F32)
-        wbias = keep.tile([P, 2], F32)
+        nx2 = keep.tile([P, 2 * M], F32)
 
         c_nats = {}
         c_grps = {}
@@ -82,12 +80,14 @@ def tile_pnn_kernel(tc, x, centers, out):
             b_t = pool.tile([P, 512], F32, tag=tag)
             return b_t
 
-        def turn_x(jp, g, tp, copy):
+        def turn_x(jp, g, tp):
             for jj in range(2):
                 for u in range(2):
                     i = jj * 2 + u
                     off = (2 * jp + jj) * 512 + 256 * g + 128 * u
                     nc.tensor.transpose(out=tp[:, i * P : (i + 1) * P], in_=xw[:, off : off + P], identity=ident[:])
+
+        def copy_x(jp, g, tp, copy):
             base = g * 2048 + jp * 512
             copy(
                 out=xg32[:, base : base + 512].rearrange("p (j r u) -> p j r u", j=2, u=2),
@@ -105,6 +105,14 @@ def tile_pnn_kernel(tc, x, centers, out):
         def square(src, acc):
             nc.scalar.activation(out=junk[:], in_=src, func=ACT.Square, accum_out=acc)
 
+        def square_v(src, acc):
+            nc.vector.scalar_tensor_tensor(
+                out=junk_v[:], in0=src, scalar=1.0, in1=src, op0=ALU.mult, op1=ALU.mult, accum_out=acc
+            )
+
+        def square_x(j, square=square):
+            square(x_nat[:, j * D : (j + 1) * D], x2[:, j : j + 1])
+
         def gram(views, dst):
             for i, v in enumerate(views):
                 nc.tensor.matmul(out=dst, lhsT=v, rhs=v, start=(i == 0), stop=(i == len(views) - 1))
@@ -120,29 +128,31 @@ def tile_pnn_kernel(tc, x, centers, out):
             nc.vector.tensor_copy(out=rep[:], in_=xm[:, h : h + 1].to_broadcast([P, P]))
             nc.tensor.transpose(out=tpx[:, 0:P], in_=rep[:], identity=ident[:])
             nc.vector.reduce_max(out=gmax[:, h : h + 1], in_=tpx[:, 0:P], axis=AX.X)
-            nc.vector.tensor_scalar_mul(out=nx2[:, h : h + 1], in0=gmax[:, h : h + 1], scalar1=-2.0)
+            for a in (0, 2):
+                nc.vector.tensor_scalar(
+                    out=nx2[:, h * M + a : h * M + a + 2],
+                    in0=gmax[:, h : h + 1].to_broadcast([P, 2]),
+                    scalar1=-2.0,
+                    scalar2=math.log(SCALE[a]),
+                    op0=ALU.mult,
+                    op1=ALU.add,
+                )
 
         def row_weights(h):
-            nc.vector.tensor_scalar(
-                out=wbias[:, h : h + 1],
-                in0=gmax[:, h : h + 1],
-                scalar1=-2.0,
-                scalar2=math.log(4.0),
-                op0=ALU.mult,
-                op1=ALU.add,
-            )
             js = slice(4 * h, 4 * h + 4)
-            nc.scalar.activation(out=w_row[:, js], in_=x2[:, js], func=ACT.Exp, scale=2.0, bias=wbias[:, h : h + 1])
+            wbias = nx2[:, h * M + 2 : h * M + 3]
+            nc.scalar.activation(out=w_row[:, js], in_=x2[:, js], func=ACT.Exp, scale=2.0, bias=wbias)
             nc.vector.tensor_scalar_max(out=w_row[:, js], in0=w_row[:, js], scalar1=2.0**-60)
 
-        def turn_c(ob, m, copy):
+        def turn_c(ob, m, tp):
             cw = c_nats[ob][:].bitcast(F32)
-            tp = ptp.tile([P, 512], F32, tag="tp")
             for g in range(2):
                 for u in range(2):
                     i = g * 2 + u
                     off = m * 512 + 256 * g + 128 * u
                     nc.tensor.transpose(out=tp[:, i * P : (i + 1) * P], in_=cw[:, off : off + P], identity=ident[:])
+
+        def copy_c(ob, m, tp, copy):
             cg32 = c_grps[ob][:].bitcast(F32)
             copy(
                 out=cg32[:, m * 512 : (m + 1) * 512].rearrange("p (g r u) -> p g r u", g=2, u=2),
@@ -150,7 +160,7 @@ def tile_pnn_kernel(tc, x, centers, out):
             )
 
         def new_c(ob):
-            c_grp = cq.tile([P, M * D], BF16, align_bytes=64)
+            c_grp = cg.tile([P, M * D], BF16, align_bytes=64)
             c_codes = cq.tile([P, M * 2 * P], U32, align_bytes=64)
             c_scales = cq.tile([P, M * 2 * P], U8, align_bytes=64)
             c_grps[ob] = c_grp
@@ -165,13 +175,15 @@ def tile_pnn_kernel(tc, x, centers, out):
                 in_=c_grps[ob][:, hf * 2048 : (hf + 1) * 2048],
             )
 
-        def square_c(ob, m):
+        def square_c(ob, m, square=square):
             square(c_nats[ob][:, m * D : (m + 1) * D], c2[:, ob * M + m : ob * M + m + 1])
 
         def gram_c(ob, ms, gr):
             for i, m in enumerate(ms):
                 col = c_grps[ob][:, m * D : (m + 1) * D].rearrange("p (g r t) -> p g t r", g=2, t=4)
                 gram([col[:, g, t, :] for g in range(2) for t in range(4)], gr[:, i * P : (i + 1) * P])
+
+        def norms_c(ob, ms, gr):
             for i, m in enumerate(ms):
                 diagonal(gr[:, i * P : (i + 1) * P], c2[:, ob * M + m : ob * M + m + 1])
 
@@ -183,16 +195,18 @@ def tile_pnn_kernel(tc, x, centers, out):
                     col = x_grp[:, a : a + 512].rearrange("p (r t) -> p t r", t=4)
                     views += [col[:, t, :] for t in range(4)]
                 gram(views, gr[:, i * P : (i + 1) * P])
+
+        def norms_x(js, gr):
             for i, j in enumerate(js):
                 diagonal(gr[:, i * P : (i + 1) * P], x2[:, j : j + 1])
 
         def biases(ob, h):
             a = h * NOB * M + ob * M
-            nc.vector.tensor_scalar(
+            nc.vector.scalar_tensor_tensor(
                 out=nbias[:, a : a + M],
                 in0=c2[:, ob * M : (ob + 1) * M],
-                scalar1=-2.0,
-                scalar2=nx2[:, h : h + 1],
+                scalar=-2.0,
+                in1=nx2[:, h * M : (h + 1) * M],
                 op0=ALU.mult,
                 op1=ALU.add,
             )
@@ -223,19 +237,21 @@ def tile_pnn_kernel(tc, x, centers, out):
 
         def tree(k, between=()):
             ob, h = k // 2, k % 2
-            p_t = p_ts[k]
+            plain = p_ts[k][:, 0 : 2 * H]
+            times4 = p_ts[k][:, 2 * H : 4 * H]
             sl = slice(ob * B + h * H, ob * B + (h + 1) * H)
-            todo = list(between)
             t_max = tr.tile([P, 2 * H], F32)
             t_sum = tr.tile([P, 2 * H], F32)
-            q_t = tr.tile([P, H], F32)
-            nc.vector.tensor_tensor(out=t_max[:], in0=p_t[:, 0 : 2 * H], in1=p_t[:, 2 * H : 4 * H], op=ALU.max)
-            nc.vector.tensor_tensor(out=t_sum[:], in0=p_t[:, 0 : 2 * H], in1=p_t[:, 2 * H : 4 * H], op=ALU.add)
-            for f in todo:
+            nc.vector.scalar_tensor_tensor(
+                out=t_max[:], in0=plain, scalar=4.0, in1=times4, op0=ALU.mult, op1=ALU.max
+            )
+            nc.vector.scalar_tensor_tensor(
+                out=t_sum[:], in0=times4, scalar=-0.25, in1=plain, op0=ALU.mult, op1=ALU.subtract
+            )
+            for f in between:
                 f()
-            nc.vector.tensor_tensor(out=q_t[:], in0=t_max[:, 0:H], in1=t_max[:, H : 2 * H], op=ALU.max)
+            nc.vector.tensor_tensor(out=q_all[:, sl], in0=t_max[:, 0:H], in1=t_max[:, H : 2 * H], op=ALU.max)
             nc.vector.tensor_tensor(out=s_all[:, sl], in0=t_sum[:, 0:H], in1=t_sum[:, H : 2 * H], op=ALU.add)
-            nc.vector.tensor_scalar_mul(out=q_all[:, sl], in0=q_t[:], scalar1=-4.0)
 
         load_x(0)
         load_x(1)
@@ -245,71 +261,104 @@ def tile_pnn_kernel(tc, x, centers, out):
         load_c(1, pieces=2)
         load_c(2)
         for j in range(3):
-            square(x_nat[:, j * D : (j + 1) * D], x2[:, j : j + 1])
+            square_x(j)
         for jp in range(2):
             for g in range(2):
-                turn_x(jp, g, bank(pmx, "acc"), nc.vector.tensor_copy)
+                tp = bank(pmx, "acc")
+                turn_x(jp, g, tp)
+                copy_x(jp, g, tp, nc.vector.tensor_copy)
         for g in range(2):
             quant_x(0, g)
         new_c(0)
         for m in range(M):
-            turn_c(0, m, nc.scalar.copy)
-        gram_x([3], bank(pgr, "gr"))
-        quant_c(0, 0)
-        shift(0, bank(pmx, "acc"))
-        square_c(0, 0)
-        gram_c(0, [1, 2, 3], bank(pmx, "acc"))
-        quant_c(0, 1)
+            tp = bank(ptp, "tp") if m < 3 else bank(pmx, "acc")
+            turn_c(0, m, tp)
+            copy_c(0, m, tp, nc.vector.tensor_copy if m < 2 else nc.scalar.copy)
+        gr_x = bank(pmx, "acc")
+        gram_x([3], gr_x)
+        for hf in range(2):
+            quant_c(0, hf)
+        norms_x([3], gr_x)
+        shift(0, bank(pgr, "gr"))
+        for m in (1, 2, 3, 0):
+            square_c(0, m, square_v if m == 1 else square)
         biases(0, 0)
-        for jp in range(2, 4):
-            for g in range(2):
-                turn_x(jp, g, bank(ptp, "tp"), nc.scalar.copy if jp == 2 else nc.vector.tensor_copy)
+        for i, (jp, g) in enumerate([(2, 0), (2, 1), (3, 0), (3, 1)]):
+            tp = bank(ptp, "tp") if i < 3 else bank(pgr, "gr")
+            turn_x(jp, g, tp)
+            copy_x(jp, g, tp, nc.vector.tensor_copy)
         for g in range(2):
             quant_x(1, g)
         products(0)
-        gram_x([4, 5, 6, 7], bank(pgr, "gr"))
+        for j in range(4, 6):
+            square_x(j)
+        gr_x = bank(pgr, "gr")
+        gram_x([7], gr_x)
+        square_x(6, square_v)
+
+        def rest_of_x():
+            norms_x([7], gr_x)
+            shift(1, bank(pgr, "gr"))
+            biases(0, 1)
+
         new_c(1)
-        turn_c(1, 0, nc.scalar.copy)
-        turn_c(1, 1, nc.scalar.copy)
-        shift(1, bank(pmx, "acc"))
-        biases(0, 1)
+        c1_banks = [bank(ptp, "tp") for m in range(3)]
+        for m in range(3):
+            turn_c(1, m, c1_banks[m])
+        tree(0, [rest_of_x])
         square_c(1, 0)
+        products(1)
+        for m in range(M):
+            copy_c(1, m, c1_banks[m], nc.vector.tensor_copy)
+            if m == 0:
+                c1_banks.append(bank(ptp, "tp"))
+                turn_c(1, 3, c1_banks[3])
+            if m == 2:
+                quant_c(1, 0)
+        quant_c(1, 1)
+        square_c(1, 1)
+        square_c(1, 2)
+        grams = {-1: (1, [3], bank(pgr, "gr"))}
 
-        def turn_step(k):
-            hf = (k + 1) % 2
-            ob = (k + 3 - hf) // 2
-            if ob >= NOB:
-                return
-            if hf == 0:
-                new_c(ob)
-            if not (hf and ob in THREE):
-                square_c(ob, 2 * hf)
-            turn_c(ob, 2 * hf, nc.scalar.copy)
-            turn_c(ob, 2 * hf + 1, nc.scalar.copy)
-
-        def quant_step(k):
-            hf = k % 2
-            ob = (k + 2 - hf) // 2
-            if ob >= NOB:
-                return
-            quant_c(ob, hf)
-            gram_c(ob, [2, 3] if hf and ob in THREE else [2 * hf + 1], bank(pgr, "gr"))
-            if hf == 1:
+        def norm_step(k):
+            if k in grams:
+                ob, ms, gr = grams[k]
+                norms_c(ob, ms, gr)
                 biases(ob, 0)
                 biases(ob, 1)
 
         for k in range(NU):
-            if k % 2 == 0 and k // 2 + 3 < NOB:
-                load_c(k // 2 + 3)
+            ob, hf = k // 2 + 2, k % 2
+            more = []
+            if ob < NOB:
+                if hf == 0:
+                    if ob + 1 < NOB:
+                        load_c(ob + 1)
+                    new_c(ob)
+                for m in (2 * hf, 2 * hf + 1):
+                    tp = bank(ptp, "tp")
+                    turn_c(ob, m, tp)
+                    copy_c(ob, m, tp, nc.vector.tensor_copy if m % 2 else nc.scalar.copy)
+                    if m < 3:
+                        square_c(ob, m)
+                more.append(lambda: quant_c(ob, hf))
             if k == 0:
-                quant_step(0)
-                turn_step(0)
+                gram_c(*grams[-1])
+            norm_step(k - 1)
+            if k + 2 < NU:
+                products(k + 2)
+            if k > 0:
+                tree(k, more)
             else:
-                turn_step(k)
-                tree(k - 1, [lambda: quant_step(k)])
-                products(k)
-            if k in (2, 3):
-                row_weights(k - 2)
+                for f in more:
+                    f()
+            if ob < NOB and hf == 1:
+                gr = bank(pgr, "gr")
+                grams[k] = (ob, [3], gr)
+                gram_c(ob, [3], gr)
+            if k == 4:
+                row_weights(0)
+                row_weights(1)
 
         l_a = keep.tile([P, 4 * O], F32, tag="xnat")
         l_b = keep.tile([P, 4 * O], F32, tag="xgrp", align_bytes=64)
@@ -331,26 +380,30 @@ def tile_pnn_kernel(tc, x, centers, out):
                         stop=(n == len(srcs) - 1),
                     )
 
+        ring = [(ptp, "tp")] * 3 + [(pgr, "gr")] + [(pmx, "acc")] * 4
+        turn = 0
         for oh in range(2):
-            if oh == 1:
-                tree(NU - 1)
             for j in range(NJ):
-                tp = bank(ptp, "tp")
-                back(tp, (s_all, q_all), j, oh)
+                b_t = bank(*ring[turn % 8])
+                turn += 1
+                back(b_t, (s_all, q_all), j, oh)
                 nc.scalar.activation(
-                    out=l_view(j, oh * H, (oh + 1) * H), in_=tp[:], func=ACT.Ln, bias=w_row[:, j : j + 1]
+                    out=l_view(j, oh * H, (oh + 1) * H), in_=b_t[:], func=ACT.Ln, scale=-1.0, bias=w_row[:, j : j + 1]
                 )
         for j in range(NJ):
-            o_t = ot.tile([P, O], F32)
+            parts = 2 if j in (0, NJ - 1) else 1
+            for i in range(parts):
+                l_p = l_view(j, i * O // parts, (i + 1) * O // parts)
+                nc.scalar.activation(out=l_p, in_=l_p, func=ACT.Exp, scale=-1.0)
             for oh in range(2):
                 l_h = l_view(j, oh * H, (oh + 1) * H)
-                nc.scalar.activation(out=l_h, in_=l_h, func=ACT.Exp, scale=-1.0)
-                acc = bank(pmx, "acc")
-                back(acc, (s_all,), j, oh)
-                nc.vector.tensor_tensor(out=o_t[:, oh * H : (oh + 1) * H], in0=acc[:], in1=l_h, op=ALU.mult)
+                b_t = bank(*ring[turn % 8])
+                turn += 1
+                back(b_t, (s_all,), j, oh)
+                nc.vector.scalar_tensor_tensor(
+                    out=l_h, in0=b_t[:], scalar=-1.0, in1=l_h, op0=ALU.mult, op1=ALU.mult
+                )
                 if j == NJ - 1:
-                    nc.sync.dma_start(
-                        out=out[j * P : (j + 1) * P, oh * H : (oh + 1) * H], in_=o_t[:, oh * H : (oh + 1) * H]
-                    )
+                    nc.sync.dma_start(out=out[j * P : (j + 1) * P, oh * H : (oh + 1) * H], in_=l_h)
             if j < NJ - 1:
-                nc.sync.dma_start(out=out[j * P : (j + 1) * P, :], in_=o_t[:])
+                nc.sync.dma_start(out=out[j * P : (j + 1) * P, :], in_=l_view(j, 0, O))

@@ -19,17 +19,19 @@ O = 1024
 M = 4
 NJ = B // P
 NOB = O // P
-NU = 2 * NOB
 H = 512
 FLOPS = 2 * B * O * M * D
+X_TURNS = ((2, 0), (2, 1), (3, 0), (3, 1))
+GRAM_NORMS = (1, 3,)
+PAIRS = 4
 SCALE = (1.0, 1.0, 4.0, 4.0)
 
 
 def tile_pnn_kernel(tc, x, centers, out):
     nc = tc.nc
-    with tc.tile_pool(name="keep", bufs=1) as keep, tc.tile_pool(name="cin", bufs=3) as cin, tc.tile_pool(
-        name="cq", bufs=3
-    ) as cq, tc.tile_pool(name="cg", bufs=2) as cg, tc.tile_pool(name="pp", bufs=4) as pp, tc.tile_pool(name="tr", bufs=2) as tr, tc.psum_pool(name="pmx", bufs=4) as pmx, tc.psum_pool(name="ptp", bufs=3) as ptp, tc.psum_pool(
+    with tc.tile_pool(name="keep", bufs=1) as keep, tc.tile_pool(name="cin", bufs=2) as cin, tc.tile_pool(
+        name="cq", bufs=2
+    ) as cq, tc.tile_pool(name="cg", bufs=2) as cg, tc.tile_pool(name="pp", bufs=3) as pp, tc.tile_pool(name="tr", bufs=1) as tr, tc.psum_pool(name="pmx", bufs=4) as pmx, tc.psum_pool(name="ptp", bufs=3) as ptp, tc.psum_pool(
         name="pgr", bufs=1
     ) as pgr, tc.manual_schedule():
         ident = keep.tile([P, P], F32)
@@ -39,7 +41,8 @@ def tile_pnn_kernel(tc, x, centers, out):
         x_grp = keep.tile([P, 2 * B * 4], BF16, tag="xgrp", align_bytes=64)
         x_codes = keep.tile([P, 2 * B], U32, align_bytes=64)
         x_scales = keep.tile([P, 2 * B], U8, align_bytes=64)
-        s_all = keep.tile([P, NOB * B], F32)
+        s_all = keep.tile([P, (NOB - PAIRS) * B], F32)
+        s_pair = keep.tile([P, PAIRS * 2 * B], F32)
         q_all = keep.tile([P, NOB * B], F32)
         junk = keep.tile([P, D], BF16)
         junk_v = keep.tile([P, D], BF16)
@@ -57,10 +60,10 @@ def tile_pnn_kernel(tc, x, centers, out):
         c_qs = {}
         p_ts = {}
 
-        def load_x(jp):
+        def load_x(j, n):
             nc.sync.dma_start(
-                out=x_nat[:, jp * 2 * D : (jp + 1) * 2 * D].rearrange("p (j k) -> p j k", j=2),
-                in_=x[jp * 2 * P : (jp + 1) * 2 * P, :].rearrange("(j p) k -> p j k", p=P),
+                out=x_nat[:, j * D : (j + n) * D].rearrange("p (j k) -> p j k", j=n),
+                in_=x[j * P : (j + n) * P, :].rearrange("(j p) k -> p j k", p=P),
             )
 
         def load_c(ob, pieces=1):
@@ -166,14 +169,9 @@ def tile_pnn_kernel(tc, x, centers, out):
             c_grps[ob] = c_grp
             c_qs[ob] = (c_codes, c_scales)
 
-        def quant_c(ob, hf):
+        def quant_c(ob):
             c_codes, c_scales = c_qs[ob]
-            cols = slice(hf * 512, (hf + 1) * 512)
-            nc.vector.quantize_mx(
-                out=c_codes[:, cols].bitcast(FP8X4),
-                scales=c_scales[:, cols],
-                in_=c_grps[ob][:, hf * 2048 : (hf + 1) * 2048],
-            )
+            nc.vector.quantize_mx(out=c_codes[:].bitcast(FP8X4), scales=c_scales[:], in_=c_grps[ob][:])
 
         def square_c(ob, m, square=square):
             square(c_nats[ob][:, m * D : (m + 1) * D], c2[:, ob * M + m : ob * M + m + 1])
@@ -200,24 +198,24 @@ def tile_pnn_kernel(tc, x, centers, out):
             for i, j in enumerate(js):
                 diagonal(gr[:, i * P : (i + 1) * P], x2[:, j : j + 1])
 
-        def biases(ob, h):
-            a = h * NOB * M + ob * M
+        def biases(ob, hs=2):
+            cols = slice(ob * M, (ob + 1) * M)
             nc.vector.scalar_tensor_tensor(
-                out=nbias[:, a : a + M],
-                in0=c2[:, ob * M : (ob + 1) * M],
+                out=nbias[:, 2 * ob * M : (2 * ob + hs) * M].rearrange("p (h m) -> p h m", m=M),
+                in0=c2[:, cols].unsqueeze(1).to_broadcast([P, hs, M]),
                 scalar=-2.0,
-                in1=nx2[:, h * M : (h + 1) * M],
+                in1=nx2[:].rearrange("p (h m) -> p h m", h=2)[:, 0:hs, :],
                 op0=ALU.mult,
                 op1=ALU.add,
             )
 
-        def products(k):
-            ob, h = k // 2, k % 2
+        def products(ob, h):
             c_codes, c_scales = c_qs[ob]
-            p_t = pp.tile([P, M * H], F32)
-            p_ts[k] = p_t
+            if h == 0:
+                p_ts[ob] = pp.tile([P, M * B], F32, name="p_t")
+            p_t = p_ts[ob]
             for m in range(M):
-                acc = pmx.tile([P, 512], F32, tag="acc")
+                acc = bank(pmx, "acc")
                 for g in range(2):
                     cs = slice((m * 2 + g) * P, (m * 2 + g + 1) * P)
                     xs = slice(g * B + h * H, g * B + (h + 1) * H)
@@ -230,37 +228,54 @@ def tile_pnn_kernel(tc, x, centers, out):
                         start=(g == 0),
                         stop=(g == 1),
                     )
-                a = h * NOB * M + ob * M + m
+                i = (2 * ob + h) * M + m
                 nc.scalar.activation(
-                    out=p_t[:, m * H : (m + 1) * H], in_=acc[:], func=ACT.Exp, scale=4.0, bias=nbias[:, a : a + 1]
+                    out=p_t[:, m * B + h * H : m * B + (h + 1) * H],
+                    in_=acc[:],
+                    func=ACT.Exp,
+                    scale=4.0,
+                    bias=nbias[:, i : i + 1],
                 )
 
-        def tree(k, between=()):
-            ob, h = k // 2, k % 2
-            plain = p_ts[k][:, 0 : 2 * H]
-            times4 = p_ts[k][:, 2 * H : 4 * H]
-            sl = slice(ob * B + h * H, ob * B + (h + 1) * H)
-            t_max = tr.tile([P, 2 * H], F32)
-            t_sum = tr.tile([P, 2 * H], F32)
+        def pair(ob):
+            return s_pair[:, ob * 2 * B : (ob + 1) * 2 * B].rearrange("p (s r) -> p s r", s=2)
+
+        def sum_parts(ob, rows):
+            if ob >= PAIRS:
+                return [s_all[:, (ob - PAIRS) * B + rows.start : (ob - PAIRS) * B + rows.stop]]
+            return [pair(ob)[:, i, rows] for i in range(2)]
+
+        def tree(ob, a, b, between=()):
+            p_v = p_ts[ob][:].rearrange("p (m r) -> p m r", m=M)
+            plain = p_v[:, 0:2, a:b]
+            times4 = p_v[:, 2:4, a:b]
+            t_max = tr.tile([P, 2, b - a], F32, name="t_max")
+            if ob >= PAIRS:
+                t_sum = tr.tile([P, 2, b - a], F32, name="t_sum")
+                sums = t_sum[:]
+            else:
+                sums = pair(ob)[:, :, a:b]
             nc.vector.scalar_tensor_tensor(
                 out=t_max[:], in0=plain, scalar=4.0, in1=times4, op0=ALU.mult, op1=ALU.max
             )
             nc.vector.scalar_tensor_tensor(
-                out=t_sum[:], in0=times4, scalar=-0.25, in1=plain, op0=ALU.mult, op1=ALU.subtract
+                out=sums, in0=times4, scalar=-0.25, in1=plain, op0=ALU.mult, op1=ALU.subtract
             )
             for f in between:
                 f()
-            nc.vector.tensor_tensor(out=q_all[:, sl], in0=t_max[:, 0:H], in1=t_max[:, H : 2 * H], op=ALU.max)
-            nc.vector.tensor_tensor(out=s_all[:, sl], in0=t_sum[:, 0:H], in1=t_sum[:, H : 2 * H], op=ALU.add)
+            sl = slice(ob * B + a, ob * B + b)
+            nc.vector.tensor_tensor(out=q_all[:, sl], in0=t_max[:, 0, :], in1=t_max[:, 1, :], op=ALU.max)
+            if ob >= PAIRS:
+                sl = slice((ob - PAIRS) * B + a, (ob - PAIRS) * B + b)
+                nc.vector.tensor_tensor(out=s_all[:, sl], in0=t_sum[:, 0, :], in1=t_sum[:, 1, :], op=ALU.add)
 
-        load_x(0)
-        load_x(1)
+        for j in range(4):
+            load_x(j, 1)
         load_c(0, pieces=2)
-        load_x(2)
-        load_x(3)
+        load_x(4, 2)
+        load_x(6, 2)
         load_c(1, pieces=2)
-        load_c(2)
-        for j in range(3):
+        for j in range(2):
             square_x(j)
         for jp in range(2):
             for g in range(2):
@@ -270,93 +285,105 @@ def tile_pnn_kernel(tc, x, centers, out):
         for g in range(2):
             quant_x(0, g)
         new_c(0)
+        square_c(0, 0)
         for m in range(M):
             tp = bank(ptp, "tp") if m < 3 else bank(pmx, "acc")
             turn_c(0, m, tp)
             copy_c(0, m, tp, nc.vector.tensor_copy if m < 2 else nc.scalar.copy)
+        for m in range(1, M):
+            square_c(0, m)
         gr_x = bank(pmx, "acc")
-        gram_x([3], gr_x)
-        for hf in range(2):
-            quant_c(0, hf)
-        norms_x([3], gr_x)
+        gram_x([2, 3], gr_x)
+        quant_c(0)
+        norms_x([2, 3], gr_x)
+        x_banks = [bank(ptp, "tp") for i in range(2)]
+        for i in range(2):
+            turn_x(*X_TURNS[i], x_banks[i])
         shift(0, bank(pgr, "gr"))
-        for m in (1, 2, 3, 0):
-            square_c(0, m, square_v if m == 1 else square)
-        biases(0, 0)
-        for i, (jp, g) in enumerate([(2, 0), (2, 1), (3, 0), (3, 1)]):
-            tp = bank(ptp, "tp") if i < 3 else bank(pgr, "gr")
-            turn_x(jp, g, tp)
-            copy_x(jp, g, tp, nc.vector.tensor_copy)
-        for g in range(2):
-            quant_x(1, g)
-        products(0)
+        biases(0, 1)
+        for i in range(2):
+            copy_x(*X_TURNS[i], x_banks[i], nc.vector.tensor_copy)
+        square_x(6, square_v)
+        products(0, 0)
         for j in range(4, 6):
             square_x(j)
+        x_banks += [bank(ptp, "tp"), bank(pgr, "gr")]
+        for i in range(2, 4):
+            turn_x(*X_TURNS[i], x_banks[i])
+        for i in range(2, 4):
+            copy_x(*X_TURNS[i], x_banks[i], nc.vector.tensor_copy)
+        for g in range(2):
+            quant_x(1, g)
+        new_c(1)
+        c1_banks = [bank(ptp, "tp") for m in range(2)]
+        for m in range(2):
+            turn_c(1, m, c1_banks[m])
         gr_x = bank(pgr, "gr")
         gram_x([7], gr_x)
-        square_x(6, square_v)
-
-        def rest_of_x():
-            norms_x([7], gr_x)
-            shift(1, bank(pgr, "gr"))
-            biases(0, 1)
-
-        new_c(1)
-        c1_banks = [bank(ptp, "tp") for m in range(3)]
-        for m in range(3):
-            turn_c(1, m, c1_banks[m])
-        tree(0, [rest_of_x])
+        norms_x([7], gr_x)
+        shift(1, bank(pgr, "gr"))
+        biases(0)
         square_c(1, 0)
-        products(1)
+        products(0, 1)
         for m in range(M):
-            copy_c(1, m, c1_banks[m], nc.vector.tensor_copy)
-            if m == 0:
+            if m >= 2:
                 c1_banks.append(bank(ptp, "tp"))
-                turn_c(1, 3, c1_banks[3])
-            if m == 2:
-                quant_c(1, 0)
-        quant_c(1, 1)
-        square_c(1, 1)
-        square_c(1, 2)
-        grams = {-1: (1, [3], bank(pgr, "gr"))}
+                turn_c(1, m, c1_banks[m])
+            copy_c(1, m, c1_banks[m], nc.vector.tensor_copy)
+        load_c(2)
+        gr = bank(pgr, "gr")
+        gram_c(1, [1], gr)
+        for m in (2, 3):
+            square_c(1, m)
+        quant_c(1)
+        norms_c(1, [1], gr)
+        biases(1)
 
-        def norm_step(k):
-            if k in grams:
-                ob, ms, gr = grams[k]
-                norms_c(ob, ms, gr)
-                biases(ob, 0)
-                biases(ob, 1)
+        def on_scalar(ob, m):
+            return m % 2 == 0 or (m == 1 and ob >= 5)
 
-        for k in range(NU):
-            ob, hf = k // 2 + 2, k % 2
-            more = []
-            if ob < NOB:
-                if hf == 0:
-                    if ob + 1 < NOB:
-                        load_c(ob + 1)
-                    new_c(ob)
-                for m in (2 * hf, 2 * hf + 1):
-                    tp = bank(ptp, "tp")
-                    turn_c(ob, m, tp)
-                    copy_c(ob, m, tp, nc.vector.tensor_copy if m % 2 else nc.scalar.copy)
-                    if m < 3:
-                        square_c(ob, m)
-                more.append(lambda: quant_c(ob, hf))
-            if k == 0:
-                gram_c(*grams[-1])
-            norm_step(k - 1)
-            if k + 2 < NU:
-                products(k + 2)
-            if k > 0:
-                tree(k, more)
+        for n in range(NOB):
+            new = n + 2
+            if new < NOB:
+                if new + 1 < NOB:
+                    load_c(new + 1)
+                new_c(new)
+                c_banks = {}
+                for m in range(3):
+                    c_banks[m] = bank(ptp, "tp")
+                    turn_c(new, m, c_banks[m])
+                scalar_copies = [m for m in range(M) if on_scalar(new, m)]
+                for m in scalar_copies[:1]:
+                    copy_c(new, m, c_banks[m], nc.scalar.copy)
+                square_c(new, 0)
+            if n + 1 < NOB:
+                products(n + 1, 0)
+            late = []
+            if new < NOB:
+                c_banks[3] = bank(ptp, "tp")
+                turn_c(new, 3, c_banks[3])
+                for m in scalar_copies[1:]:
+                    copy_c(new, m, c_banks[m], nc.scalar.copy)
+                for m in range(2, M):
+                    if m not in GRAM_NORMS:
+                        square_c(new, m)
+                for m in range(M):
+                    if m not in scalar_copies:
+                        late.append(lambda m=m: copy_c(new, m, c_banks[m], nc.vector.tensor_copy))
+                late.append(lambda: quant_c(new))
+            if n + 1 < NOB:
+                tree(n, 0, B, late)
             else:
-                for f in more:
-                    f()
-            if ob < NOB and hf == 1:
+                tree(n, 0, H)
+                tree(n, H, B)
+            if n + 1 < NOB:
+                products(n + 1, 1)
+            if new < NOB:
                 gr = bank(pgr, "gr")
-                grams[k] = (ob, [3], gr)
-                gram_c(ob, [3], gr)
-            if k == 4:
+                gram_c(new, GRAM_NORMS, gr)
+                norms_c(new, GRAM_NORMS, gr)
+                biases(new)
+            if n == 2:
                 row_weights(0)
                 row_weights(1)
 
@@ -367,13 +394,17 @@ def tile_pnn_kernel(tc, x, centers, out):
             l_t = l_a if j < 4 else l_b
             return l_t[:, (j % 4) * O + a : (j % 4) * O + b]
 
-        def back(dst, srcs, j, oh):
+        def back(dst, j, oh, with_max):
             for i in range(4):
                 ob = oh * 4 + i
+                rows = slice(j * P, (j + 1) * P)
+                srcs = sum_parts(ob, rows)
+                if with_max:
+                    srcs.append(q_all[:, ob * B + j * P : ob * B + (j + 1) * P])
                 for n, t in enumerate(srcs):
                     nc.tensor.matmul(
                         out=dst[:, i * P : (i + 1) * P],
-                        lhsT=t[:, ob * B + j * P : ob * B + (j + 1) * P],
+                        lhsT=t,
                         rhs=ident[:],
                         is_transpose=True,
                         start=(n == 0),
@@ -386,7 +417,7 @@ def tile_pnn_kernel(tc, x, centers, out):
             for j in range(NJ):
                 b_t = bank(*ring[turn % 8])
                 turn += 1
-                back(b_t, (s_all, q_all), j, oh)
+                back(b_t, j, oh, True)
                 nc.scalar.activation(
                     out=l_view(j, oh * H, (oh + 1) * H), in_=b_t[:], func=ACT.Ln, scale=-1.0, bias=w_row[:, j : j + 1]
                 )
@@ -399,7 +430,7 @@ def tile_pnn_kernel(tc, x, centers, out):
                 l_h = l_view(j, oh * H, (oh + 1) * H)
                 b_t = bank(*ring[turn % 8])
                 turn += 1
-                back(b_t, (s_all,), j, oh)
+                back(b_t, j, oh, False)
                 nc.vector.scalar_tensor_tensor(
                     out=l_h, in0=b_t[:], scalar=-1.0, in1=l_h, op0=ALU.mult, op1=ALU.mult
                 )

@@ -22,7 +22,7 @@ NOB = O // P
 H = 512
 FLOPS = 2 * B * O * M * D
 X_TURNS = ((2, 0), (2, 1), (3, 0), (3, 1))
-GRAM_NORMS = (1, 3,)
+GRAM_NORMS = ((1,),) * (NOB - 1) + ((),)
 PAIRS = 4
 SCALE = (1.0, 1.0, 4.0, 4.0)
 
@@ -51,7 +51,7 @@ def tile_pnn_kernel(tc, x, centers, out):
         c2 = keep.tile([P, NOB * M], F32)
         nbias = keep.tile([P, 2 * NOB * M], F32)
         w_row = keep.tile([P, NJ], F32)
-        xm = keep.tile([P, 2], F32)
+        logs = keep.tile([P, M], F32)
         gmax = keep.tile([P, 2], F32)
         nx2 = keep.tile([P, 2 * M], F32)
 
@@ -125,21 +125,23 @@ def tile_pnn_kernel(tc, x, centers, out):
                 out=junk_g[:], in0=src, scalar=1.0, in1=ident[:], op0=ALU.mult, op1=ALU.mult, accum_out=acc
             )
 
-        def shift(h, tpx):
-            rep = tr.tile([P, P], F32)
-            nc.vector.reduce_max(out=xm[:, h : h + 1], in_=x2[:, 4 * h : 4 * h + 4], axis=AX.X)
-            nc.vector.tensor_copy(out=rep[:], in_=xm[:, h : h + 1].to_broadcast([P, P]))
-            nc.tensor.transpose(out=tpx[:, 0:P], in_=rep[:], identity=ident[:])
-            nc.vector.reduce_max(out=gmax[:, h : h + 1], in_=tpx[:, 0:P], axis=AX.X)
-            for a in (0, 2):
-                nc.vector.tensor_scalar(
-                    out=nx2[:, h * M + a : h * M + a + 2],
-                    in0=gmax[:, h : h + 1].to_broadcast([P, 2]),
-                    scalar1=-2.0,
-                    scalar2=math.log(SCALE[a]),
-                    op0=ALU.mult,
-                    op1=ALU.add,
+        def turn_norms(h, b_t):
+            for i in range(4):
+                j = 4 * h + i
+                nc.tensor.transpose(
+                    out=b_t[:, i * P : (i + 1) * P], in_=x2[:, j : j + 1].to_broadcast([P, P]), identity=ident[:]
                 )
+
+        def shift(h, b_t):
+            nc.vector.reduce_max(out=gmax[:, h : h + 1], in_=b_t[:], axis=AX.X)
+            nc.vector.scalar_tensor_tensor(
+                out=nx2[:, h * M : (h + 1) * M],
+                in0=gmax[:, h : h + 1].to_broadcast([P, M]),
+                scalar=-2.0,
+                in1=logs[:],
+                op0=ALU.mult,
+                op1=ALU.add,
+            )
 
         def row_weights(h):
             js = slice(4 * h, 4 * h + 4)
@@ -197,6 +199,18 @@ def tile_pnn_kernel(tc, x, centers, out):
         def norms_x(js, gr):
             for i, j in enumerate(js):
                 diagonal(gr[:, i * P : (i + 1) * P], x2[:, j : j + 1])
+
+        def scalar_biases(ob):
+            for h in range(2):
+                for m in range(0, M, 2):
+                    i = (2 * ob + h) * M + m
+                    nc.scalar.activation(
+                        out=nbias[:, i : i + 2],
+                        in_=c2[:, ob * M + m : ob * M + m + 2],
+                        func=ACT.Identity,
+                        scale=-2.0,
+                        bias=nx2[:, h * M + m : h * M + m + 1],
+                    )
 
         def biases(ob, hs=2):
             cols = slice(ob * M, (ob + 1) * M)
@@ -269,6 +283,9 @@ def tile_pnn_kernel(tc, x, centers, out):
                 sl = slice((ob - PAIRS) * B + a, (ob - PAIRS) * B + b)
                 nc.vector.tensor_tensor(out=s_all[:, sl], in0=t_sum[:, 0, :], in1=t_sum[:, 1, :], op=ALU.add)
 
+        nc.vector.memset(logs[:], 0.0)
+        nc.vector.tensor_scalar_add(out=logs[:, 2:4], in0=logs[:, 2:4], scalar1=math.log(SCALE[2]))
+
         for j in range(4):
             load_x(j, 1)
         load_c(0, pieces=2)
@@ -299,10 +316,12 @@ def tile_pnn_kernel(tc, x, centers, out):
         x_banks = [bank(ptp, "tp") for i in range(2)]
         for i in range(2):
             turn_x(*X_TURNS[i], x_banks[i])
-        shift(0, bank(pgr, "gr"))
+        n_bank = bank(pgr, "gr")
+        turn_norms(0, n_bank)
+        copy_x(*X_TURNS[0], x_banks[0], nc.vector.tensor_copy)
+        shift(0, n_bank)
         biases(0, 1)
-        for i in range(2):
-            copy_x(*X_TURNS[i], x_banks[i], nc.vector.tensor_copy)
+        copy_x(*X_TURNS[1], x_banks[1], nc.vector.tensor_copy)
         square_x(6, square_v)
         products(0, 0)
         for j in range(4, 6):
@@ -321,26 +340,30 @@ def tile_pnn_kernel(tc, x, centers, out):
         gr_x = bank(pgr, "gr")
         gram_x([7], gr_x)
         norms_x([7], gr_x)
-        shift(1, bank(pgr, "gr"))
+        n_bank = bank(pgr, "gr")
+        turn_norms(1, n_bank)
+        copy_c(1, 0, c1_banks[0], nc.vector.tensor_copy)
+        shift(1, n_bank)
         biases(0)
         square_c(1, 0)
         products(0, 1)
-        for m in range(M):
+        for m in range(1, M):
             if m >= 2:
                 c1_banks.append(bank(ptp, "tp"))
                 turn_c(1, m, c1_banks[m])
             copy_c(1, m, c1_banks[m], nc.vector.tensor_copy)
         load_c(2)
         gr = bank(pgr, "gr")
-        gram_c(1, [1], gr)
-        for m in (2, 3):
-            square_c(1, m)
+        gram_c(1, GRAM_NORMS[1], gr)
+        for m in range(1, M):
+            if m not in GRAM_NORMS[1]:
+                square_c(1, m)
         quant_c(1)
-        norms_c(1, [1], gr)
+        norms_c(1, GRAM_NORMS[1], gr)
         biases(1)
 
         def on_scalar(ob, m):
-            return m % 2 == 0 or (m == 1 and ob >= 5)
+            return m == 0 or (m == 2 and ob >= 6)
 
         for n in range(NOB):
             new = n + 2
@@ -355,7 +378,9 @@ def tile_pnn_kernel(tc, x, centers, out):
                 scalar_copies = [m for m in range(M) if on_scalar(new, m)]
                 for m in scalar_copies[:1]:
                     copy_c(new, m, c_banks[m], nc.scalar.copy)
-                square_c(new, 0)
+                for m in range(2):
+                    if m not in GRAM_NORMS[new]:
+                        square_c(new, m)
             if n + 1 < NOB:
                 products(n + 1, 0)
             late = []
@@ -365,7 +390,7 @@ def tile_pnn_kernel(tc, x, centers, out):
                 for m in scalar_copies[1:]:
                     copy_c(new, m, c_banks[m], nc.scalar.copy)
                 for m in range(2, M):
-                    if m not in GRAM_NORMS:
+                    if m not in GRAM_NORMS[new]:
                         square_c(new, m)
                 for m in range(M):
                     if m not in scalar_copies:
@@ -378,11 +403,13 @@ def tile_pnn_kernel(tc, x, centers, out):
                 tree(n, H, B)
             if n + 1 < NOB:
                 products(n + 1, 1)
-            if new < NOB:
+            if new < NOB and GRAM_NORMS[new]:
                 gr = bank(pgr, "gr")
-                gram_c(new, GRAM_NORMS, gr)
-                norms_c(new, GRAM_NORMS, gr)
+                gram_c(new, GRAM_NORMS[new], gr)
+                norms_c(new, GRAM_NORMS[new], gr)
                 biases(new)
+            elif new < NOB:
+                scalar_biases(new)
             if n == 2:
                 row_weights(0)
                 row_weights(1)
@@ -422,19 +449,30 @@ def tile_pnn_kernel(tc, x, centers, out):
                     out=l_view(j, oh * H, (oh + 1) * H), in_=b_t[:], func=ACT.Ln, scale=-1.0, bias=w_row[:, j : j + 1]
                 )
         for j in range(NJ):
-            parts = 2 if j in (0, NJ - 1) else 1
-            for i in range(parts):
-                l_p = l_view(j, i * O // parts, (i + 1) * O // parts)
-                nc.scalar.activation(out=l_p, in_=l_p, func=ACT.Exp, scale=-1.0)
+            if j == 0:
+                cuts = [0, H, O]
+            elif j < NJ - 1:
+                cuts = [0, O]
+            else:
+                cuts = [0, H, O - H // 2, O]
+            for a, b in zip(cuts[:-1], cuts[1:]):
+                nc.scalar.activation(out=l_view(j, a, b), in_=l_view(j, a, b), func=ACT.Exp, scale=-1.0)
             for oh in range(2):
-                l_h = l_view(j, oh * H, (oh + 1) * H)
                 b_t = bank(*ring[turn % 8])
                 turn += 1
                 back(b_t, j, oh, False)
-                nc.vector.scalar_tensor_tensor(
-                    out=l_h, in0=b_t[:], scalar=-1.0, in1=l_h, op0=ALU.mult, op1=ALU.mult
-                )
-                if j == NJ - 1:
-                    nc.sync.dma_start(out=out[j * P : (j + 1) * P, oh * H : (oh + 1) * H], in_=l_h)
+                edges = [c for c in cuts if oh * H < c < (oh + 1) * H]
+                edges = [oh * H] + edges + [(oh + 1) * H]
+                for a, b in zip(edges[:-1], edges[1:]):
+                    nc.vector.scalar_tensor_tensor(
+                        out=l_view(j, a, b),
+                        in0=b_t[:, a - oh * H : b - oh * H],
+                        scalar=-1.0,
+                        in1=l_view(j, a, b),
+                        op0=ALU.mult,
+                        op1=ALU.mult,
+                    )
+                    if j == NJ - 1:
+                        nc.sync.dma_start(out=out[j * P : (j + 1) * P, a:b], in_=l_view(j, a, b))
             if j < NJ - 1:
                 nc.sync.dma_start(out=out[j * P : (j + 1) * P, :], in_=l_view(j, 0, O))

@@ -23,7 +23,7 @@ H = 512
 FLOPS = 2 * B * O * M * D
 X_TURNS = ((2, 0), (2, 1), (3, 0), (3, 1))
 GRAM_NORMS = ((1,),) * (NOB - 1) + ((),)
-PAIRS = 4
+GPSIMD_ROWS = 768
 SCALE = (1.0, 1.0, 4.0, 4.0)
 
 
@@ -41,8 +41,7 @@ def tile_pnn_kernel(tc, x, centers, out):
         x_grp = keep.tile([P, 2 * B * 4], BF16, tag="xgrp", align_bytes=64)
         x_codes = keep.tile([P, 2 * B], U32, align_bytes=64)
         x_scales = keep.tile([P, 2 * B], U8, align_bytes=64)
-        s_all = keep.tile([P, (NOB - PAIRS) * B], F32)
-        s_pair = keep.tile([P, PAIRS * 2 * B], F32)
+        s_all = keep.tile([P, NOB * B], F32)
         q_all = keep.tile([P, NOB * B], F32)
         junk = keep.tile([P, D], BF16)
         junk_v = keep.tile([P, D], BF16)
@@ -251,37 +250,38 @@ def tile_pnn_kernel(tc, x, centers, out):
                     bias=nbias[:, i : i + 1],
                 )
 
-        def pair(ob):
-            return s_pair[:, ob * 2 * B : (ob + 1) * 2 * B].rearrange("p (s r) -> p s r", s=2)
-
-        def sum_parts(ob, rows):
-            if ob >= PAIRS:
-                return [s_all[:, (ob - PAIRS) * B + rows.start : (ob - PAIRS) * B + rows.stop]]
-            return [pair(ob)[:, i, rows] for i in range(2)]
-
         def tree(ob, a, b, between=()):
             p_v = p_ts[ob][:].rearrange("p (m r) -> p m r", m=M)
             plain = p_v[:, 0:2, a:b]
             times4 = p_v[:, 2:4, a:b]
             t_max = tr.tile([P, 2, b - a], F32, name="t_max")
-            if ob >= PAIRS:
-                t_sum = tr.tile([P, 2, b - a], F32, name="t_sum")
-                sums = t_sum[:]
-            else:
-                sums = pair(ob)[:, :, a:b]
+            t_sum = tr.tile([P, 2, b - a], F32, name="t_sum")
             nc.vector.scalar_tensor_tensor(
                 out=t_max[:], in0=plain, scalar=4.0, in1=times4, op0=ALU.mult, op1=ALU.max
             )
             nc.vector.scalar_tensor_tensor(
-                out=sums, in0=times4, scalar=-0.25, in1=plain, op0=ALU.mult, op1=ALU.subtract
+                out=t_sum[:], in0=times4, scalar=-0.25, in1=plain, op0=ALU.mult, op1=ALU.subtract
             )
+            split = a
+            if b - a == B:
+                split = a + GPSIMD_ROWS
+                nc.gpsimd.tensor_tensor(
+                    out=s_all[:, ob * B + a : ob * B + split],
+                    in0=t_sum[:, 0, 0 : split - a],
+                    in1=t_sum[:, 1, 0 : split - a],
+                    op=ALU.add,
+                )
             for f in between:
                 f()
             sl = slice(ob * B + a, ob * B + b)
             nc.vector.tensor_tensor(out=q_all[:, sl], in0=t_max[:, 0, :], in1=t_max[:, 1, :], op=ALU.max)
-            if ob >= PAIRS:
-                sl = slice((ob - PAIRS) * B + a, (ob - PAIRS) * B + b)
-                nc.vector.tensor_tensor(out=s_all[:, sl], in0=t_sum[:, 0, :], in1=t_sum[:, 1, :], op=ALU.add)
+            if split < b:
+                nc.vector.tensor_tensor(
+                    out=s_all[:, ob * B + split : ob * B + b],
+                    in0=t_sum[:, 0, split - a :],
+                    in1=t_sum[:, 1, split - a :],
+                    op=ALU.add,
+                )
 
         nc.vector.memset(logs[:], 0.0)
         nc.vector.tensor_scalar_add(out=logs[:, 2:4], in0=logs[:, 2:4], scalar1=math.log(SCALE[2]))
@@ -363,7 +363,7 @@ def tile_pnn_kernel(tc, x, centers, out):
         biases(1)
 
         def on_scalar(ob, m):
-            return m == 0 or (m == 2 and ob >= 6)
+            return m == 0
 
         for n in range(NOB):
             new = n + 2
@@ -421,17 +421,13 @@ def tile_pnn_kernel(tc, x, centers, out):
             l_t = l_a if j < 4 else l_b
             return l_t[:, (j % 4) * O + a : (j % 4) * O + b]
 
-        def back(dst, j, oh, with_max):
+        def back(dst, srcs, j, oh):
             for i in range(4):
                 ob = oh * 4 + i
-                rows = slice(j * P, (j + 1) * P)
-                srcs = sum_parts(ob, rows)
-                if with_max:
-                    srcs.append(q_all[:, ob * B + j * P : ob * B + (j + 1) * P])
                 for n, t in enumerate(srcs):
                     nc.tensor.matmul(
                         out=dst[:, i * P : (i + 1) * P],
-                        lhsT=t,
+                        lhsT=t[:, ob * B + j * P : ob * B + (j + 1) * P],
                         rhs=ident[:],
                         is_transpose=True,
                         start=(n == 0),
@@ -444,7 +440,7 @@ def tile_pnn_kernel(tc, x, centers, out):
             for j in range(NJ):
                 b_t = bank(*ring[turn % 8])
                 turn += 1
-                back(b_t, j, oh, True)
+                back(b_t, (s_all, q_all), j, oh)
                 nc.scalar.activation(
                     out=l_view(j, oh * H, (oh + 1) * H), in_=b_t[:], func=ACT.Ln, scale=-1.0, bias=w_row[:, j : j + 1]
                 )
@@ -460,7 +456,7 @@ def tile_pnn_kernel(tc, x, centers, out):
             for oh in range(2):
                 b_t = bank(*ring[turn % 8])
                 turn += 1
-                back(b_t, j, oh, False)
+                back(b_t, (s_all,), j, oh)
                 edges = [c for c in cuts if oh * H < c < (oh + 1) * H]
                 edges = [oh * H] + edges + [(oh + 1) * H]
                 for a, b in zip(edges[:-1], edges[1:]):

@@ -250,20 +250,26 @@ def tile_pnn_kernel(tc, x, centers, out):
                     bias=nbias[:, i : i + 1],
                 )
 
-        def tree(ob, a, b, between=()):
+        def halves(ob, a, b):
             p_v = p_ts[ob][:].rearrange("p (m r) -> p m r", m=M)
-            plain = p_v[:, 0:2, a:b]
-            times4 = p_v[:, 2:4, a:b]
+            return p_v[:, 0:2, a:b], p_v[:, 2:4, a:b]
+
+        def tree_max(ob, a, b):
+            plain, times4 = halves(ob, a, b)
             t_max = tr.tile([P, 2, b - a], F32, name="t_max")
-            t_sum = tr.tile([P, 2, b - a], F32, name="t_sum")
             nc.vector.scalar_tensor_tensor(
                 out=t_max[:], in0=plain, scalar=4.0, in1=times4, op0=ALU.mult, op1=ALU.max
             )
+            return t_max
+
+        def tree(ob, a, b, t_max, between=()):
+            plain, times4 = halves(ob, a, b)
+            t_sum = tr.tile([P, 2, b - a], F32, name="t_sum")
             nc.vector.scalar_tensor_tensor(
                 out=t_sum[:], in0=times4, scalar=-0.25, in1=plain, op0=ALU.mult, op1=ALU.subtract
             )
             split = a
-            if b - a == B:
+            if b - a == B and ob + 2 < NOB:
                 split = a + GPSIMD_ROWS
                 nc.gpsimd.tensor_tensor(
                     out=s_all[:, ob * B + a : ob * B + split],
@@ -302,55 +308,55 @@ def tile_pnn_kernel(tc, x, centers, out):
         for g in range(2):
             quant_x(0, g)
         new_c(0)
-        square_c(0, 0)
+        square_x(2)
         for m in range(M):
             tp = bank(ptp, "tp") if m < 3 else bank(pmx, "acc")
             turn_c(0, m, tp)
             copy_c(0, m, tp, nc.vector.tensor_copy if m < 2 else nc.scalar.copy)
-        for m in range(1, M):
-            square_c(0, m)
         gr_x = bank(pmx, "acc")
-        gram_x([2, 3], gr_x)
+        gram_x([3], gr_x)
         quant_c(0)
-        norms_x([2, 3], gr_x)
+        norms_x([3], gr_x)
         x_banks = [bank(ptp, "tp") for i in range(2)]
         for i in range(2):
             turn_x(*X_TURNS[i], x_banks[i])
         n_bank = bank(pgr, "gr")
         turn_norms(0, n_bank)
-        copy_x(*X_TURNS[0], x_banks[0], nc.vector.tensor_copy)
+        for m in (1, 0, 2, 3):
+            square_c(0, m, square_v if m == 1 else square)
         shift(0, n_bank)
+        copy_x(*X_TURNS[0], x_banks[0], nc.vector.tensor_copy)
         biases(0, 1)
         copy_x(*X_TURNS[1], x_banks[1], nc.vector.tensor_copy)
         square_x(6, square_v)
         products(0, 0)
-        for j in range(4, 6):
+        for j in (4, 7):
             square_x(j)
         x_banks += [bank(ptp, "tp"), bank(pgr, "gr")]
         for i in range(2, 4):
             turn_x(*X_TURNS[i], x_banks[i])
+        gr_x = bank(pmx, "acc")
+        gram_x([5], gr_x)
         for i in range(2, 4):
             copy_x(*X_TURNS[i], x_banks[i], nc.vector.tensor_copy)
         for g in range(2):
             quant_x(1, g)
+        norms_x([5], gr_x)
         new_c(1)
-        c1_banks = [bank(ptp, "tp") for m in range(2)]
-        for m in range(2):
+        c1_banks = [bank(ptp, "tp") for m in range(3)]
+        for m in range(3):
             turn_c(1, m, c1_banks[m])
-        gr_x = bank(pgr, "gr")
-        gram_x([7], gr_x)
-        norms_x([7], gr_x)
         n_bank = bank(pgr, "gr")
         turn_norms(1, n_bank)
         copy_c(1, 0, c1_banks[0], nc.vector.tensor_copy)
         shift(1, n_bank)
+        copy_c(1, 1, c1_banks[1], nc.vector.tensor_copy)
         biases(0)
         square_c(1, 0)
         products(0, 1)
-        for m in range(1, M):
-            if m >= 2:
-                c1_banks.append(bank(ptp, "tp"))
-                turn_c(1, m, c1_banks[m])
+        c1_banks.append(bank(ptp, "tp"))
+        turn_c(1, 3, c1_banks[3])
+        for m in range(2, M):
             copy_c(1, m, c1_banks[m], nc.vector.tensor_copy)
         load_c(2)
         gr = bank(pgr, "gr")
@@ -359,11 +365,47 @@ def tile_pnn_kernel(tc, x, centers, out):
             if m not in GRAM_NORMS[1]:
                 square_c(1, m)
         quant_c(1)
+        t_max = tree_max(0, 0, B)
         norms_c(1, GRAM_NORMS[1], gr)
         biases(1)
 
         def on_scalar(ob, m):
-            return m == 0
+            return m == 0 or (m == 2 and ob == 7)
+
+        l_a = keep.tile([P, 4 * O], F32, tag="xnat")
+        l_b = keep.tile([P, 4 * O], F32, tag="xgrp", align_bytes=64)
+
+        def l_view(j, a, b):
+            l_t = l_a if j < 4 else l_b
+            return l_t[:, (j % 4) * O + a : (j % 4) * O + b]
+
+        def back(dst, srcs, j, obs):
+            for ob in obs:
+                i = ob % 4
+                for n, t in enumerate(srcs):
+                    nc.tensor.matmul(
+                        out=dst[:, i * P : (i + 1) * P],
+                        lhsT=t[:, ob * B + j * P : ob * B + (j + 1) * P],
+                        rhs=ident[:],
+                        is_transpose=True,
+                        start=(n == 0),
+                        stop=(n == len(srcs) - 1),
+                    )
+
+        ring = [(pgr, "gr")] + [(ptp, "tp")] * 3 + [(pmx, "acc")] * 4
+        early = []
+
+        def next_bank():
+            n_bank = turned[0] % len(ring)
+            turned[0] += 1
+            return bank(*ring[n_bank])
+
+        def back_bank(j, oh, with_max):
+            b_t = next_bank()
+            back(b_t, (s_all, q_all) if with_max else (s_all,), j, range(oh * 4, oh * 4 + 4))
+            return b_t
+
+        turned = [0]
 
         for n in range(NOB):
             new = n + 2
@@ -381,6 +423,8 @@ def tile_pnn_kernel(tc, x, centers, out):
                 for m in range(2):
                     if m not in GRAM_NORMS[new]:
                         square_c(new, m)
+            if n + 2 == NOB:
+                early += [back_bank(j, 0, True) for j in range(4)]
             if n + 1 < NOB:
                 products(n + 1, 0)
             late = []
@@ -397,10 +441,10 @@ def tile_pnn_kernel(tc, x, centers, out):
                         late.append(lambda m=m: copy_c(new, m, c_banks[m], nc.vector.tensor_copy))
                 late.append(lambda: quant_c(new))
             if n + 1 < NOB:
-                tree(n, 0, B, late)
+                tree(n, 0, B, tree_max(n, 0, B) if n > 0 else t_max, late)
             else:
-                tree(n, 0, H)
-                tree(n, H, B)
+                for h in range(2):
+                    tree(n, h * H, (h + 1) * H, tree_max(n, h * H, (h + 1) * H))
             if n + 1 < NOB:
                 products(n + 1, 1)
             if new < NOB and GRAM_NORMS[new]:
@@ -414,33 +458,17 @@ def tile_pnn_kernel(tc, x, centers, out):
                 row_weights(0)
                 row_weights(1)
 
-        l_a = keep.tile([P, 4 * O], F32, tag="xnat")
-        l_b = keep.tile([P, 4 * O], F32, tag="xgrp", align_bytes=64)
-
-        def l_view(j, a, b):
-            l_t = l_a if j < 4 else l_b
-            return l_t[:, (j % 4) * O + a : (j % 4) * O + b]
-
-        def back(dst, srcs, j, oh):
-            for i in range(4):
-                ob = oh * 4 + i
-                for n, t in enumerate(srcs):
-                    nc.tensor.matmul(
-                        out=dst[:, i * P : (i + 1) * P],
-                        lhsT=t[:, ob * B + j * P : ob * B + (j + 1) * P],
-                        rhs=ident[:],
-                        is_transpose=True,
-                        start=(n == 0),
-                        stop=(n == len(srcs) - 1),
-                    )
-
-        ring = [(ptp, "tp")] * 3 + [(pgr, "gr")] + [(pmx, "acc")] * 4
-        turn = 0
         for oh in range(2):
             for j in range(NJ):
-                b_t = bank(*ring[turn % 8])
-                turn += 1
-                back(b_t, (s_all, q_all), j, oh)
+                if oh == 0:
+                    b_t = early[j] if j < len(early) else back_bank(j, oh, True)
+                else:
+                    if j % 4 == 0:
+                        late = [next_bank() for i in range(4)]
+                        for obs in (range(4, NOB - 1), range(NOB - 1, NOB)):
+                            for i in range(4):
+                                back(late[i], (s_all, q_all), j + i, obs)
+                    b_t = late[j % 4]
                 nc.scalar.activation(
                     out=l_view(j, oh * H, (oh + 1) * H), in_=b_t[:], func=ACT.Ln, scale=-1.0, bias=w_row[:, j : j + 1]
                 )
@@ -454,9 +482,7 @@ def tile_pnn_kernel(tc, x, centers, out):
             for a, b in zip(cuts[:-1], cuts[1:]):
                 nc.scalar.activation(out=l_view(j, a, b), in_=l_view(j, a, b), func=ACT.Exp, scale=-1.0)
             for oh in range(2):
-                b_t = bank(*ring[turn % 8])
-                turn += 1
-                back(b_t, (s_all,), j, oh)
+                b_t = back_bank(j, oh, False)
                 edges = [c for c in cuts if oh * H < c < (oh + 1) * H]
                 edges = [oh * H] + edges + [(oh + 1) * H]
                 for a, b in zip(edges[:-1], edges[1:]):

@@ -23,7 +23,7 @@ H = 512
 FLOPS = 2 * B * O * M * D
 X_TURNS = ((2, 0), (2, 1), (3, 0), (3, 1))
 GRAM_NORMS = ((1,),) * (NOB - 1) + ((),)
-GPSIMD_ROWS = 768
+PAIRS = 2
 SCALE = (1.0, 1.0, 4.0, 4.0)
 
 
@@ -41,7 +41,8 @@ def tile_pnn_kernel(tc, x, centers, out):
         x_grp = keep.tile([P, 2 * B * 4], BF16, tag="xgrp", align_bytes=64)
         x_codes = keep.tile([P, 2 * B], U32, align_bytes=64)
         x_scales = keep.tile([P, 2 * B], U8, align_bytes=64)
-        s_all = keep.tile([P, NOB * B], F32)
+        s_all = keep.tile([P, (NOB - PAIRS) * B], F32)
+        s_pair = keep.tile([P, PAIRS * 2 * B], F32)
         q_all = keep.tile([P, NOB * B], F32)
         junk = keep.tile([P, D], BF16)
         junk_v = keep.tile([P, D], BF16)
@@ -250,6 +251,9 @@ def tile_pnn_kernel(tc, x, centers, out):
                     bias=nbias[:, i : i + 1],
                 )
 
+        def pair(ob):
+            return s_pair[:, ob * 2 * B : (ob + 1) * 2 * B].rearrange("p (s r) -> p s r", s=2)
+
         def halves(ob, a, b):
             p_v = p_ts[ob][:].rearrange("p (m r) -> p m r", m=M)
             return p_v[:, 0:2, a:b], p_v[:, 2:4, a:b]
@@ -264,30 +268,21 @@ def tile_pnn_kernel(tc, x, centers, out):
 
         def tree(ob, a, b, t_max, between=()):
             plain, times4 = halves(ob, a, b)
-            t_sum = tr.tile([P, 2, b - a], F32, name="t_sum")
+            if ob < PAIRS:
+                sums = pair(ob)[:, :, a:b]
+            else:
+                t_sum = tr.tile([P, 2, b - a], F32, name="t_sum")
+                sums = t_sum[:]
             nc.vector.scalar_tensor_tensor(
-                out=t_sum[:], in0=times4, scalar=-0.25, in1=plain, op0=ALU.mult, op1=ALU.subtract
+                out=sums, in0=times4, scalar=-0.25, in1=plain, op0=ALU.mult, op1=ALU.subtract
             )
-            split = a
-            if b - a == B and ob + 2 < NOB:
-                split = a + GPSIMD_ROWS
-                nc.gpsimd.tensor_tensor(
-                    out=s_all[:, ob * B + a : ob * B + split],
-                    in0=t_sum[:, 0, 0 : split - a],
-                    in1=t_sum[:, 1, 0 : split - a],
-                    op=ALU.add,
-                )
             for f in between:
                 f()
             sl = slice(ob * B + a, ob * B + b)
             nc.vector.tensor_tensor(out=q_all[:, sl], in0=t_max[:, 0, :], in1=t_max[:, 1, :], op=ALU.max)
-            if split < b:
-                nc.vector.tensor_tensor(
-                    out=s_all[:, ob * B + split : ob * B + b],
-                    in0=t_sum[:, 0, split - a :],
-                    in1=t_sum[:, 1, split - a :],
-                    op=ALU.add,
-                )
+            if ob >= PAIRS:
+                sl = slice((ob - PAIRS) * B + a, (ob - PAIRS) * B + b)
+                nc.vector.tensor_tensor(out=s_all[:, sl], in0=t_sum[:, 0, :], in1=t_sum[:, 1, :], op=ALU.add)
 
         nc.vector.memset(logs[:], 0.0)
         nc.vector.tensor_scalar_add(out=logs[:, 2:4], in0=logs[:, 2:4], scalar1=math.log(SCALE[2]))
@@ -370,7 +365,7 @@ def tile_pnn_kernel(tc, x, centers, out):
         biases(1)
 
         def on_scalar(ob, m):
-            return m == 0 or (m == 2 and ob == 7)
+            return m == 0 or (m == 2 and ob >= 5)
 
         l_a = keep.tile([P, 4 * O], F32, tag="xnat")
         l_b = keep.tile([P, 4 * O], F32, tag="xgrp", align_bytes=64)
@@ -379,13 +374,22 @@ def tile_pnn_kernel(tc, x, centers, out):
             l_t = l_a if j < 4 else l_b
             return l_t[:, (j % 4) * O + a : (j % 4) * O + b]
 
-        def back(dst, srcs, j, obs):
+        def parts(ob, j):
+            rows = slice(j * P, (j + 1) * P)
+            if ob < PAIRS:
+                return [pair(ob)[:, i, rows] for i in range(2)]
+            return [s_all[:, (ob - PAIRS) * B + j * P : (ob - PAIRS) * B + (j + 1) * P]]
+
+        def back(dst, with_max, j, obs):
             for ob in obs:
                 i = ob % 4
+                srcs = parts(ob, j)
+                if with_max:
+                    srcs.append(q_all[:, ob * B + j * P : ob * B + (j + 1) * P])
                 for n, t in enumerate(srcs):
                     nc.tensor.matmul(
                         out=dst[:, i * P : (i + 1) * P],
-                        lhsT=t[:, ob * B + j * P : ob * B + (j + 1) * P],
+                        lhsT=t,
                         rhs=ident[:],
                         is_transpose=True,
                         start=(n == 0),
@@ -402,7 +406,7 @@ def tile_pnn_kernel(tc, x, centers, out):
 
         def back_bank(j, oh, with_max):
             b_t = next_bank()
-            back(b_t, (s_all, q_all) if with_max else (s_all,), j, range(oh * 4, oh * 4 + 4))
+            back(b_t, with_max, j, range(oh * 4, oh * 4 + 4))
             return b_t
 
         turned = [0]
@@ -428,6 +432,7 @@ def tile_pnn_kernel(tc, x, centers, out):
             if n + 1 < NOB:
                 products(n + 1, 0)
             late = []
+            copies = []
             if new < NOB:
                 c_banks[3] = bank(ptp, "tp")
                 turn_c(new, 3, c_banks[3])
@@ -438,10 +443,14 @@ def tile_pnn_kernel(tc, x, centers, out):
                         square_c(new, m)
                 for m in range(M):
                     if m not in scalar_copies:
-                        late.append(lambda m=m: copy_c(new, m, c_banks[m], nc.vector.tensor_copy))
+                        copies.append(m)
                 late.append(lambda: quant_c(new))
             if n + 1 < NOB:
-                tree(n, 0, B, tree_max(n, 0, B) if n > 0 else t_max, late)
+                if n > 0:
+                    t_max = tree_max(n, 0, B)
+                for m in copies:
+                    copy_c(new, m, c_banks[m], nc.vector.tensor_copy)
+                tree(n, 0, B, t_max, late)
             else:
                 for h in range(2):
                     tree(n, h * H, (h + 1) * H, tree_max(n, h * H, (h + 1) * H))
@@ -467,7 +476,7 @@ def tile_pnn_kernel(tc, x, centers, out):
                         late = [next_bank() for i in range(4)]
                         for obs in (range(4, NOB - 1), range(NOB - 1, NOB)):
                             for i in range(4):
-                                back(late[i], (s_all, q_all), j + i, obs)
+                                back(late[i], True, j + i, obs)
                     b_t = late[j % 4]
                 nc.scalar.activation(
                     out=l_view(j, oh * H, (oh + 1) * H), in_=b_t[:], func=ACT.Ln, scale=-1.0, bias=w_row[:, j : j + 1]

import math

import concourse.mybir as mybir
from concourse.masks import make_identity

F32 = mybir.dt.float32
BF16 = mybir.dt.bfloat16
U32 = mybir.dt.uint32
U8 = mybir.dt.uint8
FP8X4 = mybir.dt.float8_e4m3fn_x4
ACT = mybir.ActivationFunctionType
ALU = mybir.AluOpType
AX = mybir.AxisListType

P = 128
B = 1024
D = 1024
O = 1024
M = 4
NJ = B // P
NOB = O // P
H = 512
FLOPS = 2 * B * O * M * D
X_TURNS = ((2, 0), (2, 1), (3, 0), (3, 1))
GRAM_NORMS = ((1,),) * (NOB - 1) + ((),)
PAIRS = 2
SCALE = (1.0, 1.0, 4.0, 4.0)


def tile_pnn_kernel(tc, x, centers, out):
    nc = tc.nc
    with tc.tile_pool(name="keep", bufs=1) as keep, tc.tile_pool(name="cin", bufs=2) as cin, tc.tile_pool(
        name="cq", bufs=2
    ) as cq, tc.tile_pool(name="cg", bufs=2) as cg, tc.tile_pool(name="pp", bufs=3) as pp, tc.tile_pool(name="tr", bufs=1) as tr, tc.psum_pool(name="pmx", bufs=4) as pmx, tc.psum_pool(name="ptp", bufs=3) as ptp, tc.psum_pool(
        name="pgr", bufs=1
    ) as pgr, tc.manual_schedule():
        ident = keep.tile([P, P], F32)
        make_identity(nc, ident[:])

        x_nat = keep.tile([P, NJ * D], BF16, tag="xnat")
        x_grp = keep.tile([P, 2 * B * 4], BF16, tag="xgrp", align_bytes=64)
        x_codes = keep.tile([P, 2 * B], U32, align_bytes=64)
        x_scales = keep.tile([P, 2 * B], U8, align_bytes=64)
        s_all = keep.tile([P, (NOB - PAIRS) * B], F32)
        s_pair = keep.tile([P, PAIRS * 2 * B], F32)
        q_all = keep.tile([P, NOB * B], F32)
        junk = keep.tile([P, D], BF16)
        junk_v = keep.tile([P, D], BF16)
        junk_g = keep.tile([P, P], F32)
        x2 = keep.tile([P, NJ], F32)
        c2 = keep.tile([P, NOB * M], F32)
        nbias = keep.tile([P, 2 * NOB * M], F32)
        w_row = keep.tile([P, NJ], F32)
        logs = keep.tile([P, M], F32)
        gmax = keep.tile([P, 2], F32)
        nx2 = keep.tile([P, 2 * M], F32)

        c_nats = {}
        c_grps = {}
        c_qs = {}
        p_ts = {}

        def load_x(j, n):
            nc.sync.dma_start(
                out=x_nat[:, j * D : (j + n) * D].rearrange("p (j k) -> p j k", j=n),
                in_=x[j * P : (j + n) * P, :].rearrange("(j p) k -> p j k", p=P),
            )

        def load_c(ob, pieces=1):
            c_nat = cin.tile([P, M * D], BF16)
            n = M // pieces
            for i in range(pieces):
                nc.sync.dma_start(
                    out=c_nat[:, i * n * D : (i + 1) * n * D].rearrange("p (m k) -> p m k", m=n),
                    in_=centers[ob * P : (ob + 1) * P, i * n : (i + 1) * n, :],
                )
            c_nats[ob] = c_nat

        xw = x_nat[:].bitcast(F32)
        xg32 = x_grp[:].bitcast(F32)

        def bank(pool, tag):
            b_t = pool.tile([P, 512], F32, tag=tag)
            return b_t

        def turn_x(jp, g, tp):
            for jj in range(2):
                for u in range(2):
                    i = jj * 2 + u
                    off = (2 * jp + jj) * 512 + 256 * g + 128 * u
                    nc.tensor.transpose(out=tp[:, i * P : (i + 1) * P], in_=xw[:, off : off + P], identity=ident[:])

        def copy_x(jp, g, tp, copy):
            base = g * 2048 + jp * 512
            copy(
                out=xg32[:, base : base + 512].rearrange("p (j r u) -> p j r u", j=2, u=2),
                in_=tp[:].rearrange("p (j u r) -> p j r u", j=2, u=2),
            )

        def quant_x(h, g):
            cols = slice(g * B + h * H, g * B + (h + 1) * H)
            nc.vector.quantize_mx(
                out=x_codes[:, cols].bitcast(FP8X4),
                scales=x_scales[:, cols],
                in_=x_grp[:, 4 * (g * B + h * H) : 4 * (g * B + (h + 1) * H)],
            )

        def square(src, acc):
            nc.scalar.activation(out=junk[:], in_=src, func=ACT.Square, accum_out=acc)

        def square_v(src, acc):
            nc.vector.scalar_tensor_tensor(
                out=junk_v[:], in0=src, scalar=1.0, in1=src, op0=ALU.mult, op1=ALU.mult, accum_out=acc
            )

        def square_x(j, square=square):
            square(x_nat[:, j * D : (j + 1) * D], x2[:, j : j + 1])

        def gram(views, dst):
            for i, v in enumerate(views):
                nc.tensor.matmul(out=dst, lhsT=v, rhs=v, start=(i == 0), stop=(i == len(views) - 1))

        def diagonal(src, acc):
            nc.vector.scalar_tensor_tensor(
                out=junk_g[:], in0=src, scalar=1.0, in1=ident[:], op0=ALU.mult, op1=ALU.mult, accum_out=acc
            )

        def turn_norms(h, b_t):
            for i in range(4):
                j = 4 * h + i
                nc.tensor.transpose(
                    out=b_t[:, i * P : (i + 1) * P], in_=x2[:, j : j + 1].to_broadcast([P, P]), identity=ident[:]
                )

        def shift(h, b_t):
            nc.vector.reduce_max(out=gmax[:, h : h + 1], in_=b_t[:], axis=AX.X)
            nc.vector.scalar_tensor_tensor(
                out=nx2[:, h * M : (h + 1) * M],
                in0=gmax[:, h : h + 1].to_broadcast([P, M]),
                scalar=-2.0,
                in1=logs[:],
                op0=ALU.mult,
                op1=ALU.add,
            )

        def row_weights(h):
            js = slice(4 * h, 4 * h + 4)
            wbias = nx2[:, h * M + 2 : h * M + 3]
            nc.scalar.activation(out=w_row[:, js], in_=x2[:, js], func=ACT.Exp, scale=2.0, bias=wbias)
            nc.vector.tensor_scalar_max(out=w_row[:, js], in0=w_row[:, js], scalar1=2.0**-60)

        def turn_c(ob, m, tp):
            cw = c_nats[ob][:].bitcast(F32)
            for g in range(2):
                for u in range(2):
                    i = g * 2 + u
                    off = m * 512 + 256 * g + 128 * u
                    nc.tensor.transpose(out=tp[:, i * P : (i + 1) * P], in_=cw[:, off : off + P], identity=ident[:])

        def copy_c(ob, m, tp, copy):
            cg32 = c_grps[ob][:].bitcast(F32)
            copy(
                out=cg32[:, m * 512 : (m + 1) * 512].rearrange("p (g r u) -> p g r u", g=2, u=2),
                in_=tp[:].rearrange("p (g u r) -> p g r u", g=2, u=2),
            )

        def new_c(ob):
            c_grp = cg.tile([P, M * D], BF16, align_bytes=64)
            c_codes = cq.tile([P, M * 2 * P], U32, align_bytes=64)
            c_scales = cq.tile([P, M * 2 * P], U8, align_bytes=64)
            c_grps[ob] = c_grp
            c_qs[ob] = (c_codes, c_scales)

        def quant_c(ob):
            c_codes, c_scales = c_qs[ob]
            nc.vector.quantize_mx(out=c_codes[:].bitcast(FP8X4), scales=c_scales[:], in_=c_grps[ob][:])

        def square_c(ob, m, square=square):
            square(c_nats[ob][:, m * D : (m + 1) * D], c2[:, ob * M + m : ob * M + m + 1])

        def gram_c(ob, ms, gr):
            for i, m in enumerate(ms):
                col = c_grps[ob][:, m * D : (m + 1) * D].rearrange("p (g r t) -> p g t r", g=2, t=4)
                gram([col[:, g, t, :] for g in range(2) for t in range(4)], gr[:, i * P : (i + 1) * P])

        def norms_c(ob, ms, gr):
            for i, m in enumerate(ms):
                diagonal(gr[:, i * P : (i + 1) * P], c2[:, ob * M + m : ob * M + m + 1])

        def gram_x(js, gr):
            for i, j in enumerate(js):
                views = []
                for g in range(2):
                    a = g * 4 * B + j * 512
                    col = x_grp[:, a : a + 512].rearrange("p (r t) -> p t r", t=4)
                    views += [col[:, t, :] for t in range(4)]
                gram(views, gr[:, i * P : (i + 1) * P])

        def norms_x(js, gr):
            for i, j in enumerate(js):
                diagonal(gr[:, i * P : (i + 1) * P], x2[:, j : j + 1])

        def scalar_biases(ob):
            for h in range(2):
                for m in range(0, M, 2):
                    i = (2 * ob + h) * M + m
                    nc.scalar.activation(
                        out=nbias[:, i : i + 2],
                        in_=c2[:, ob * M + m : ob * M + m + 2],
                        func=ACT.Identity,
                        scale=-2.0,
                        bias=nx2[:, h * M + m : h * M + m + 1],
                    )

        def biases(ob, hs=2):
            cols = slice(ob * M, (ob + 1) * M)
            nc.vector.scalar_tensor_tensor(
                out=nbias[:, 2 * ob * M : (2 * ob + hs) * M].rearrange("p (h m) -> p h m", m=M),
                in0=c2[:, cols].unsqueeze(1).to_broadcast([P, hs, M]),
                scalar=-2.0,
                in1=nx2[:].rearrange("p (h m) -> p h m", h=2)[:, 0:hs, :],
                op0=ALU.mult,
                op1=ALU.add,
            )

        def products(ob, h):
            c_codes, c_scales = c_qs[ob]
            if h == 0:
                p_ts[ob] = pp.tile([P, M * B], F32, name="p_t")
            p_t = p_ts[ob]
            for m in range(M):
                acc = bank(pmx, "acc")
                for g in range(2):
                    cs = slice((m * 2 + g) * P, (m * 2 + g + 1) * P)
                    xs = slice(g * B + h * H, g * B + (h + 1) * H)
                    nc.tensor.matmul_mx(
                        out=acc[:],
                        lhsT=c_codes[:, cs].bitcast(FP8X4),
                        lhsT_scale=c_scales[:, cs],
                        rhs=x_codes[:, xs].bitcast(FP8X4),
                        rhs_scale=x_scales[:, xs],
                        start=(g == 0),
                        stop=(g == 1),
                    )
                i = (2 * ob + h) * M + m
                nc.scalar.activation(
                    out=p_t[:, m * B + h * H : m * B + (h + 1) * H],
                    in_=acc[:],
                    func=ACT.Exp,
                    scale=4.0,
                    bias=nbias[:, i : i + 1],
                )

        def pair(ob):
            return s_pair[:, ob * 2 * B : (ob + 1) * 2 * B].rearrange("p (s r) -> p s r", s=2)

        def halves(ob, a, b):
            p_v = p_ts[ob][:].rearrange("p (m r) -> p m r", m=M)
            return p_v[:, 0:2, a:b], p_v[:, 2:4, a:b]

        def tree_max(ob, a, b):
            plain, times4 = halves(ob, a, b)
            t_max = tr.tile([P, 2, b - a], F32, name="t_max")
            nc.vector.scalar_tensor_tensor(
                out=t_max[:], in0=plain, scalar=4.0, in1=times4, op0=ALU.mult, op1=ALU.max
            )
            return t_max

        def tree(ob, a, b, t_max, between=()):
            plain, times4 = halves(ob, a, b)
            if ob < PAIRS:
                sums = pair(ob)[:, :, a:b]
            else:
                t_sum = tr.tile([P, 2, b - a], F32, name="t_sum")
                sums = t_sum[:]
            nc.vector.scalar_tensor_tensor(
                out=sums, in0=times4, scalar=-0.25, in1=plain, op0=ALU.mult, op1=ALU.subtract
            )
            for f in between:
                f()
            sl = slice(ob * B + a, ob * B + b)
            nc.vector.tensor_tensor(out=q_all[:, sl], in0=t_max[:, 0, :], in1=t_max[:, 1, :], op=ALU.max)
            if ob >= PAIRS:
                sl = slice((ob - PAIRS) * B + a, (ob - PAIRS) * B + b)
                nc.vector.tensor_tensor(out=s_all[:, sl], in0=t_sum[:, 0, :], in1=t_sum[:, 1, :], op=ALU.add)

        nc.vector.memset(logs[:], 0.0)
        nc.vector.tensor_scalar_add(out=logs[:, 2:4], in0=logs[:, 2:4], scalar1=math.log(SCALE[2]))

        for j in range(4):
            load_x(j, 1)
        load_c(0, pieces=2)
        load_x(4, 2)
        load_x(6, 2)
        load_c(1, pieces=2)
        for j in range(2):
            square_x(j)
        for jp in range(2):
            for g in range(2):
                tp = bank(pmx, "acc")
                turn_x(jp, g, tp)
                copy_x(jp, g, tp, nc.vector.tensor_copy)
        for g in range(2):
            quant_x(0, g)
        new_c(0)
        square_x(2)
        for m in range(M):
            tp = bank(ptp, "tp") if m < 3 else bank(pmx, "acc")
            turn_c(0, m, tp)
            copy_c(0, m, tp, nc.vector.tensor_copy if m < 2 else nc.scalar.copy)
        gr_x = bank(pmx, "acc")
        gram_x([3], gr_x)
        quant_c(0)
        norms_x([3], gr_x)
        x_banks = [bank(ptp, "tp") for i in range(2)]
        for i in range(2):
            turn_x(*X_TURNS[i], x_banks[i])
        n_bank = bank(pgr, "gr")
        turn_norms(0, n_bank)
        for m in (1, 0, 2, 3):
            square_c(0, m, square_v if m == 1 else square)
        shift(0, n_bank)
        copy_x(*X_TURNS[0], x_banks[0], nc.vector.tensor_copy)
        biases(0, 1)
        copy_x(*X_TURNS[1], x_banks[1], nc.vector.tensor_copy)
        square_x(6, square_v)
        products(0, 0)
        for j in (4, 7):
            square_x(j)
        x_banks += [bank(ptp, "tp"), bank(pgr, "gr")]
        for i in range(2, 4):
            turn_x(*X_TURNS[i], x_banks[i])
        gr_x = bank(pmx, "acc")
        gram_x([5], gr_x)
        for i in range(2, 4):
            copy_x(*X_TURNS[i], x_banks[i], nc.vector.tensor_copy)
        for g in range(2):
            quant_x(1, g)
        norms_x([5], gr_x)
        new_c(1)
        c1_banks = [bank(ptp, "tp") for m in range(3)]
        for m in range(3):
            turn_c(1, m, c1_banks[m])
        n_bank = bank(pgr, "gr")
        turn_norms(1, n_bank)
        copy_c(1, 0, c1_banks[0], nc.vector.tensor_copy)
        shift(1, n_bank)
        copy_c(1, 1, c1_banks[1], nc.vector.tensor_copy)
        biases(0)
        square_c(1, 0)
        products(0, 1)
        c1_banks.append(bank(ptp, "tp"))
        turn_c(1, 3, c1_banks[3])
        for m in range(2, M):
            copy_c(1, m, c1_banks[m], nc.vector.tensor_copy)
        load_c(2)
        gr = bank(pgr, "gr")
        gram_c(1, GRAM_NORMS[1], gr)
        for m in range(1, M):
            if m not in GRAM_NORMS[1]:
                square_c(1, m)
        quant_c(1)
        t_max = tree_max(0, 0, B)
        norms_c(1, GRAM_NORMS[1], gr)
        biases(1)

        def on_scalar(ob, m):
            return m == 0 or (m == 2 and ob >= 5)

        l_a = keep.tile([P, 4 * O], F32, tag="xnat")
        l_b = keep.tile([P, 4 * O], F32, tag="xgrp", align_bytes=64)

        def l_view(j, a, b):
            l_t = l_a if j < 4 else l_b
            return l_t[:, (j % 4) * O + a : (j % 4) * O + b]

        def parts(ob, j):
            rows = slice(j * P, (j + 1) * P)
            if ob < PAIRS:
                return [pair(ob)[:, i, rows] for i in range(2)]
            return [s_all[:, (ob - PAIRS) * B + j * P : (ob - PAIRS) * B + (j + 1) * P]]

        def back(dst, with_max, j, obs):
            for ob in obs:
                i = ob % 4
                srcs = parts(ob, j)
                if with_max:
                    srcs.append(q_all[:, ob * B + j * P : ob * B + (j + 1) * P])
                for n, t in enumerate(srcs):
                    nc.tensor.matmul(
                        out=dst[:, i * P : (i + 1) * P],
                        lhsT=t,
                        rhs=ident[:],
                        is_transpose=True,
                        start=(n == 0),
                        stop=(n == len(srcs) - 1),
                    )

        ring = [(pgr, "gr")] + [(ptp, "tp")] * 3 + [(pmx, "acc")] * 4
        early = []

        def next_bank():
            n_bank = turned[0] % len(ring)
            turned[0] += 1
            return bank(*ring[n_bank])

        def back_bank(j, oh, with_max):
            b_t = next_bank()
            back(b_t, with_max, j, range(oh * 4, oh * 4 + 4))
            return b_t

        turned = [0]

        for n in range(NOB):
            new = n + 2
            if new < NOB:
                if new + 1 < NOB:
                    load_c(new + 1)
                new_c(new)
                c_banks = {}
                for m in range(3):
                    c_banks[m] = bank(ptp, "tp")
                    turn_c(new, m, c_banks[m])
                scalar_copies = [m for m in range(M) if on_scalar(new, m)]
                for m in scalar_copies[:1]:
                    copy_c(new, m, c_banks[m], nc.scalar.copy)
                for m in range(2):
                    if m not in GRAM_NORMS[new]:
                        square_c(new, m)
            if n + 2 == NOB:
                early += [back_bank(j, 0, True) for j in range(4)]
            if n + 1 < NOB:
                products(n + 1, 0)
            late = []
            copies = []
            if new < NOB:
                c_banks[3] = bank(ptp, "tp")
                turn_c(new, 3, c_banks[3])
                for m in scalar_copies[1:]:
                    copy_c(new, m, c_banks[m], nc.scalar.copy)
                for m in range(2, M):
                    if m not in GRAM_NORMS[new]:
                        square_c(new, m)
                for m in range(M):
                    if m not in scalar_copies:
                        copies.append(m)
                late.append(lambda: quant_c(new))
            if n + 1 < NOB:
                if n > 0:
                    t_max = tree_max(n, 0, B)
                for m in copies:
                    copy_c(new, m, c_banks[m], nc.vector.tensor_copy)
                tree(n, 0, B, t_max, late)
            else:
                for h in range(2):
                    tree(n, h * H, (h + 1) * H, tree_max(n, h * H, (h + 1) * H))
            if n + 1 < NOB:
                products(n + 1, 1)
            if new < NOB and GRAM_NORMS[new]:
                gr = bank(pgr, "gr")
                gram_c(new, GRAM_NORMS[new], gr)
                norms_c(new, GRAM_NORMS[new], gr)
                biases(new)
            elif new < NOB:
                scalar_biases(new)
            if n == 2:
                row_weights(0)
                row_weights(1)

        for oh in range(2):
            for j in range(NJ):
                if oh == 0:
                    b_t = early[j] if j < len(early) else back_bank(j, oh, True)
                else:
                    if j % 4 == 0:
                        late = [next_bank() for i in range(4)]
                        for obs in (range(4, NOB - 1), range(NOB - 1, NOB)):
                            for i in range(4):
                                back(late[i], True, j + i, obs)
                    b_t = late[j % 4]
                nc.scalar.activation(
                    out=l_view(j, oh * H, (oh + 1) * H), in_=b_t[:], func=ACT.Ln, scale=-1.0, bias=w_row[:, j : j + 1]
                )
        for j in range(NJ):
            if j == 0:
                cuts = [0, H, O]
            elif j < NJ - 1:
                cuts = [0, O]
            else:
                cuts = [0, H, O - H // 2, O]
            for a, b in zip(cuts[:-1], cuts[1:]):
                nc.scalar.activation(out=l_view(j, a, b), in_=l_view(j, a, b), func=ACT.Exp, scale=-1.0)
            for oh in range(2):
                b_t = back_bank(j, oh, False)
                edges = [c for c in cuts if oh * H < c < (oh + 1) * H]
                edges = [oh * H] + edges + [(oh + 1) * H]
                for a, b in zip(edges[:-1], edges[1:]):
                    nc.vector.scalar_tensor_tensor(
                        out=l_view(j, a, b),
                        in0=b_t[:, a - oh * H : b - oh * H],
                        scalar=-1.0,
                        in1=l_view(j, a, b),
                        op0=ALU.mult,
                        op1=ALU.mult,
                    )
                    if j == NJ - 1:
                        nc.sync.dma_start(out=out[j * P : (j + 1) * P, a:b], in_=l_view(j, a, b))
            if j < NJ - 1:
                nc.sync.dma_start(out=out[j * P : (j + 1) * P, :], in_=l_view(j, 0, O))
